import numpy as np
import ml_dtypes


def mxq(x, axis, fmt="e4m3"):
    dtype, down = {"e4m3": (ml_dtypes.float8_e4m3fn, 7), "e5m2": (ml_dtypes.float8_e5m2, 14)}[fmt]
    v = np.moveaxis(np.asarray(x, np.float32).astype(ml_dtypes.bfloat16).astype(np.float64), axis, -1)
    blocks = v.reshape(v.shape[:-1] + (-1, 32))
    amax = np.abs(blocks).max(-1, keepdims=True)
    byte = np.maximum(np.where(amax > 0, np.frexp(amax)[1] - 1 + 127, 0) - down, 1)
    scale = np.exp2(byte - 127.0)
    codes = (blocks / scale).astype(np.float32).astype(dtype).astype(np.float64)
    return np.moveaxis((codes * scale).reshape(v.shape), -1, axis)


WIDE = False


def mx_kscale(k):
    if not WIDE:
        return np.ones(k)
    levels = np.array([10, -10, 5, -5, 0])
    a = np.random.permutation(np.resize(levels, k // 512 * 4)).reshape(k // 512, 4)
    idx = np.arange(k)
    return np.exp2(a[idx // 512, idx % 128 // 32])


BF16 = ml_dtypes.bfloat16


def bf(x):
    return np.asarray(x, np.float32).astype(BF16)


def f64(x):
    return np.asarray(x).astype(np.float64)


E2M1 = np.array([0.0, 0.5, 1.0, 1.5, 2.0, 3.0, 4.0, 6.0, -0.0, -0.5, -1.0, -1.5, -2.0, -3.0, -4.0, -6.0])


def pack_weight(w, fmt):
    k, n = w.shape
    w = f64(bf(w)).reshape(k // 32, 32, n)
    amax = np.abs(w).max(1)
    if fmt == "e4m3":
        byte = np.frexp(amax)[1] - 1 + 127 - 7
    else:
        mant, ex = np.frexp(amax / 6.0)
        byte = np.where(mant > 0.5, ex, ex - 1) + 127
    byte = np.clip(np.where(amax > 0, byte, 1), 1, 254)
    scaled = (w * np.exp2(127.0 - byte)[:, None, :]).reshape(k, n).astype(np.float32)
    by_word = np.ascontiguousarray(scaled.reshape(k // 512, 128, 4, n).transpose(0, 1, 3, 2))
    if fmt == "e4m3":
        words = by_word.astype(ml_dtypes.float8_e4m3fn).view(np.uint8)
    else:
        c = by_word.astype(ml_dtypes.float4_e2m1fn).view(np.uint8) & 0xF
        words = c[..., 0::2] | (c[..., 1::2] << 4)
    return np.ascontiguousarray(words), np.ascontiguousarray(byte.astype(np.uint8).reshape(k // 512, 16, n))


def unpack_weight(words, scales, fmt):
    g, p, n, _ = words.shape
    if fmt == "e4m3":
        vals = np.ascontiguousarray(words).view(ml_dtypes.float8_e4m3fn).astype(np.float64)
    else:
        nib = np.empty((g, p, n, 4), np.uint8)
        nib[..., 0::2] = words & 0xF
        nib[..., 1::2] = words >> 4
        vals = E2M1[nib]
    vals = vals * np.repeat(np.exp2(scales.astype(np.float64) - 127.0), 8, axis=1)[..., None]
    return vals.transpose(0, 1, 3, 2).reshape(g * 512, n)

def pack4(w):
    words, scales = pack_weight(w, "e2m1")
    return words.reshape(words.shape[0], 128, -1), scales


def unpack4(words, scales):
    return unpack_weight(words.reshape(words.shape[0], 128, -1, 2), scales, "e2m1")


B, N, D1, D2, NS = 64, 16, 1024, 256, 2
ND = D1
NP = N // NS


def rolled_concat(arrays, n, axis=-1):
    return np.concatenate(arrays[n:] + arrays[:n], axis=axis)


def setup_inputs():
    t = mx_kscale(NS * D2)
    tb = t.reshape(NS, D2)
    fac = np.stack([np.roll(tb, i, axis=0) for i in range(NS)])
    x2 = np.random.standard_normal((B, NS, NP, NS, NP, D2)) * fac[None, :, None, :, None, :]
    in_1e = bf(np.random.standard_normal((B, N, D1)))
    in_2e = bf(x2.reshape(B, N, N, D2))
    wu_words, wu_scales = pack4(np.random.standard_normal((D1, ND)) * 0.6 / np.sqrt(D1))
    b_unmixed = bf(np.random.standard_normal(ND) * 0.3)
    wm_words, wm_scales = pack4(np.random.standard_normal((NS * D1, ND)) * 0.6 * np.sqrt(NP) / np.sqrt(NS * D1))
    w2_words, w2_scales = pack4(np.random.standard_normal((NS * D2, ND)) * 0.6 * np.sqrt(NP) / np.sqrt(NS * D2) / t[:, None])
    return {"in_1e": in_1e,
            "in_2e": in_2e,
            "W_unmixed_words": wu_words,
            "W_unmixed_scales": wu_scales,
            "b_unmixed": b_unmixed,
            "W_mixed_words": wm_words,
            "W_mixed_scales": wm_scales,
            "W_2e_words": w2_words,
            "W_2e_scales": w2_scales}


def reference(in_1e, in_2e, W_unmixed_words, W_unmixed_scales, b_unmixed, W_mixed_words, W_mixed_scales, W_2e_words, W_2e_scales):
    x1, x2 = f64(in_1e), f64(in_2e)
    dense_unmixed = (mxq(x1, 2, "e4m3") @ unpack4(W_unmixed_words, W_unmixed_scales)) + f64(b_unmixed)
    split_unmixed = np.split(dense_unmixed, NS, axis=-2)
    split_1e = np.split(x1, NS, axis=-2)
    split_means = [np.mean(s, axis=-2, keepdims=True) for s in split_1e]
    split_concat = [rolled_concat(split_means, i) for i in range(NS)]
    all_spins = np.concatenate(split_concat, axis=-2)
    dense_mixed = mxq(all_spins, 2, "e4m3") @ unpack4(W_mixed_words, W_mixed_scales)
    dense_mixed_split = np.split(dense_mixed, NS, axis=-2)
    split_2e = np.split(x2, NS, axis=-3)
    concat_2e = []
    for spin in range(NS):
        blocks = np.split(split_2e[spin], NS, axis=-2)
        means = [np.mean(p, axis=-2) for p in blocks]
        concat_2e.append(rolled_concat(means, spin))
    all_2e = np.concatenate(concat_2e, axis=-2)
    dense_2e = mxq(all_2e, 2, "e4m3") @ unpack4(W_2e_words, W_2e_scales)
    dense_2e_split = np.split(dense_2e, NS, axis=-2)
    out_splits = [u + m + e for u, m, e in zip(split_unmixed, dense_mixed_split, dense_2e_split)]
    dense_out = np.concatenate(out_splits, axis=-2)
    return np.tanh(dense_out) + x1

@@ -1,0 +1,307 @@
+from contextlib import ExitStack
+
+import concourse.mybir as mybir
+from concourse.masks import make_identity
+
+F32 = mybir.dt.float32
+BF16 = mybir.dt.bfloat16
+I32 = mybir.dt.int32
+U32 = mybir.dt.uint32
+U8 = mybir.dt.uint8
+FP8X4 = mybir.dt.float8_e4m3fn_x4
+FP4X4 = mybir.dt.float4_e2m1fn_x4
+ADD = mybir.AluOpType.add
+ACT = mybir.ActivationFunctionType
+
+P = 128
+WALKERS = 64
+SPINS = 2
+RANKS = 8
+D1 = 1024
+D2 = 256
+N_HALF = 512
+HALVES = D1 // N_HALF
+K_PASS = 512
+GROUPS = 8
+GROUP_TOKENS = P // GROUPS
+
+PASS_UNMIXED = 0
+PASS_MIXED = 2
+PASS_2E = 6
+PASSES = 7
+
+FLOPS = 2 * (WALKERS * 16 * D1 * D1 + WALKERS * SPINS * SPINS * D1 * D1 + WALKERS * 16 * SPINS * D2 * D1)
+
+
+def tile_ferminetoneelectronlayer_pa_kernel(
+    tc,
+    in_1e,
+    in_2e,
+    w_unmixed_words,
+    w_unmixed_scales,
+    b_unmixed,
+    w_mixed_words,
+    w_mixed_scales,
+    w_2e_words,
+    w_2e_scales,
+    out,
+):
+    nc = tc.nc
+    with ExitStack() as ctx:
+        const = ctx.enter_context(tc.tile_pool(name="const", bufs=1))
+        keep = ctx.enter_context(tc.tile_pool(name="keep", bufs=1))
+        pair_pool = ctx.enter_context(tc.tile_pool(name="pair_pool", bufs=RANKS))
+        out_pool = ctx.enter_context(tc.tile_pool(name="out_pool", bufs=RANKS))
+        work = ctx.enter_context(tc.tile_pool(name="work", bufs=2))
+        psum_sums = ctx.enter_context(tc.psum_pool(name="psum_sums", bufs=2))
+        psum_flip = ctx.enter_context(tc.psum_pool(name="psum_flip", bufs=3))
+        psum_acc = ctx.enter_context(tc.psum_pool(name="psum_acc", bufs=3))
+        totals_pool = ctx.enter_context(tc.tile_pool(name="totals_pool", bufs=4))
+        ctx.enter_context(tc.manual_schedule())
+
+        x1_rows = in_1e.flatten_outer_dims().rearrange("(q r) k -> q r k", r=RANKS)
+        out_rows = out.flatten_outer_dims().rearrange("(q r) n -> q r n", r=RANKS)
+        pair_rows = in_2e.rearrange("b (s r) (c j a) d -> (b s) r (c j) (a d)", s=SPINS, c=SPINS, a=2)
+
+        w_scales = keep.tile([P, PASSES, D1], U8, align_bytes=64)
+        nc.vector.memset(w_scales[:].bitcast(I32), 0)
+        bias_row = keep.tile([P, D1], BF16)
+        nc.vector.memset(bias_row[:], 0.0)
+        ident_bf = const.tile([P, P], BF16)
+        make_identity(nc, ident_bf[:])
+        ident_f32 = const.tile([P, P], F32)
+        make_identity(nc, ident_f32[:])
+        swap = const.tile([P, P], BF16)
+        for s in range(SPINS):
+            nc.vector.tensor_copy(
+                out=swap[:].rearrange("p (b s) -> p b s", s=SPINS)[:, :, s],
+                in_=ident_bf[:].rearrange("p (b s) -> p b s", s=SPINS)[:, :, 1 - s],
+            )
+        ones = const.tile([P, P], BF16)
+        nc.vector.memset(ones[:], 1.0)
+        member = const.tile([P, 2 * GROUP_TOKENS], F32)
+        nc.vector.tensor_reduce(
+            out=member[:],
+            in_=ident_bf[:].rearrange("p (g j) -> p g j", j=4),
+            axis=mybir.AxisListType.X,
+            op=ADD,
+        )
+        averager = const.tile([P, SPINS, GROUP_TOKENS], BF16)
+        for s in range(SPINS):
+            for o in range(SPINS):
+                nc.vector.tensor_scalar_mul(
+                    out=averager[:].rearrange("p o (b s) -> p o b s", s=SPINS)[:, o, :, s],
+                    in0=member[:].rearrange("p (b s c) -> p b s c", s=SPINS, c=SPINS)[:, :, s, (o + s) % SPINS],
+                    scalar1=1.0 / RANKS,
+                )
+
+        w_words = keep.tile([P, PASSES, 2 * D1], U8, align_bytes=64)
+        x1 = keep.tile([P, RANKS, D1], BF16)
+        pair_tiles = []
+
+        def load_scales(first, scales):
+            passes = scales.shape[0]
+            for quadrant in range(4):
+                nc.sync.dma_start(
+                    out=w_scales[32 * quadrant : 32 * quadrant + 4, first : first + passes, :].bitcast(I32),
+                    in_=scales[:, 4 * quadrant : 4 * quadrant + 4, :].rearrange("g r n -> r g n").bitcast(I32),
+                )
+
+        def load_words(first, words):
+            passes = words.shape[0]
+            nc.sync.dma_start(
+                out=w_words[:, first : first + passes, :].bitcast(I32),
+                in_=words.rearrange("g p n -> p g n").bitcast(I32),
+            )
+
+        def load_pairs(r):
+            pairs = pair_pool.tile([P, GROUPS, 2 * D2], BF16)
+            for grp in range(GROUPS):
+                nc.sync.dma_start(
+                    out=pairs[:, grp, :],
+                    in_=pair_rows[GROUP_TOKENS * grp : GROUP_TOKENS * (grp + 1), r],
+                )
+            pair_tiles.append(pairs)
+
+        for r in range(0, RANKS, 2):
+            nc.sync.dma_start(out=x1[:, r : r + 2, :], in_=x1_rows[:, r : r + 2, :])
+        load_pairs(0)
+        load_scales(PASS_MIXED, w_mixed_scales)
+        load_scales(PASS_UNMIXED, w_unmixed_scales)
+        load_scales(PASS_2E, w_2e_scales)
+        nc.sync.dma_start(out=bias_row[0:1, :], in_=b_unmixed.unsqueeze(0))
+        load_words(PASS_MIXED, w_mixed_words)
+        load_pairs(1)
+        load_words(PASS_UNMIXED, w_unmixed_words)
+        load_words(PASS_2E, w_2e_words)
+        for r in range(2, RANKS):
+            load_pairs(r)
+
+        def mx_pass(acc, codes, scales, w_pass, half, start, stop):
+            nc.tensor.matmul_mx(
+                out=acc,
+                lhsT=codes.bitcast(FP8X4),
+                lhsT_scale=scales,
+                rhs=w_words[:, w_pass, 2 * N_HALF * half : 2 * N_HALF * (half + 1)].bitcast(FP4X4),
+                rhs_scale=w_scales[:, w_pass, N_HALF * half : N_HALF * (half + 1)],
+                start=start,
+                stop=stop,
+            )
+
+        x1_codes = keep.tile([P, RANKS, 2 * P], U32, align_bytes=64)
+        x1_scales = keep.tile([P, RANKS, 2 * P], U8, align_bytes=64)
+        sums = keep.tile([P, 4, D1], F32)
+
+        def flip_x1(r):
+            x1_words = x1[:, r, :].bitcast(F32)
+            flipped = psum_flip.tile([P, 2, 2, P], F32, tag="flip")
+            for g in range(2):
+                for u in range(2):
+                    nc.tensor.transpose(
+                        flipped[:, g, u, :],
+                        x1_words[:, 256 * g + u : 256 * (g + 1) : 2],
+                        ident_f32[:],
+                    )
+            x1_grouped = work.tile([P, 2 * K_PASS], BF16, align_bytes=64)
+            nc.scalar.copy(
+                out=x1_grouped[:].bitcast(F32).rearrange("p (g q u) -> p g q u", g=2, u=2),
+                in_=flipped[:].rearrange("p g u q -> p g q u"),
+            )
+            return x1_grouped
+
+        for c in range(4):
+            grouped_pair = [flip_x1(2 * c), flip_x1(2 * c + 1)]
+            nc.vector.tensor_tensor(out=sums[:, c, :], in0=x1[:, 2 * c, :], in1=x1[:, 2 * c + 1, :], op=ADD)
+            for i in range(2):
+                nc.vector.quantize_mx(
+                    out=x1_codes[:, 2 * c + i, :].bitcast(FP8X4),
+                    scales=x1_scales[:, 2 * c + i, :],
+                    in_=grouped_pair[i][:],
+                )
+
+        pair_codes = keep.tile([P, RANKS, P], U32, align_bytes=64)
+        pair_scales = keep.tile([P, RANKS, P], U8, align_bytes=64)
+        mixed = keep.tile([P, D1], F32)
+        pair_means_of = {}
+        sorted_k_of = {}
+
+        def average_pairs(r):
+            pairs = pair_tiles[r]
+            pair_sums = psum_sums.tile([P, 2, SPINS, GROUPS, GROUP_TOKENS], F32)
+            for grp in range(GROUPS):
+                for h in range(2):
+                    for a in range(2):
+                        nc.tensor.matmul(
+                            out=pair_sums[:, h, :, grp, :],
+                            lhsT=pairs[:, grp, D2 * a + P * h : D2 * a + P * (h + 1)],
+                            rhs=averager[:],
+                            start=(a == 0),
+                            stop=(a == 1),
+                        )
+            pair_means = work.tile([P, 2, SPINS, P], BF16)
+            nc.scalar.copy(out=pair_means[:], in_=pair_sums[:].rearrange("p h o g q -> p h o (g q)"))
+            pair_means_of[r] = pair_means
+
+        def tokens_to_partitions(r):
+            pair_means = pair_means_of[r]
+            by_token = psum_flip.tile([P, SPINS, 2, P], BF16, tag="flip")
+            for o in range(SPINS):
+                for h in range(2):
+                    nc.tensor.transpose(by_token[:, o, h, :], pair_means[:, h, o, :], ident_bf[:])
+            sorted_k = work.tile([P, 4, P], BF16)
+            nc.scalar.copy(
+                out=sorted_k[:],
+                in_=by_token[:].rearrange("q o h d -> q (o h d)").rearrange("q (p t) -> q t p", t=4),
+            )
+            sorted_k_of[r] = sorted_k
+
+        def quantise_pairs(r):
+            sorted_k = sorted_k_of[r]
+            flipped = psum_flip.tile([P, 4, P], BF16, tag="flip")
+            for t in range(4):
+                nc.tensor.transpose(flipped[:, t, :], sorted_k[:, t, :], ident_bf[:])
+            pair_grouped = work.tile([P, P, 4], BF16, align_bytes=64)
+            nc.vector.tensor_copy(out=pair_grouped[:], in_=flipped[:].rearrange("p t q -> p q t"))
+            nc.vector.quantize_mx(
+                out=pair_codes[:, r, :].bitcast(FP8X4),
+                scales=pair_scales[:, r, :],
+                in_=pair_grouped[:].rearrange("p q t -> p (q t)"),
+            )
+
+        def finish(r):
+            result = out_pool.tile([P, D1], F32)
+            totals = []
+            for half in range(HALVES):
+                acc = psum_acc.tile([P, N_HALF], F32, tag="acc")
+                for g in range(2):
+                    mx_pass(
+                        acc[:],
+                        x1_codes[:, r, P * g : P * (g + 1)],
+                        x1_scales[:, r, P * g : P * (g + 1)],
+                        PASS_UNMIXED + g,
+                        half,
+                        g == 0,
+                        False,
+                    )
+                mx_pass(acc[:], pair_codes[:, r, :], pair_scales[:, r, :], PASS_2E, half, False, True)
+                total = totals_pool.tile([P, N_HALF], F32)
+                nc.vector.tensor_tensor(
+                    out=total[:], in0=acc[:], in1=mixed[:, N_HALF * half : N_HALF * (half + 1)], op=ADD
+                )
+                nc.scalar.activation(out=total[:], in_=total[:], func=ACT.Tanh)
+                totals.append(total)
+            for half in range(HALVES):
+                cols = slice(N_HALF * half, N_HALF * (half + 1))
+                nc.gpsimd.tensor_tensor(out=result[:, cols], in0=totals[half][:], in1=x1[:, r, cols], op=ADD)
+            nc.sync.dma_start(out=out_rows[:, r, :], in_=result[:])
+
+        average_pairs(0)
+
+        nc.vector.tensor_tensor(out=sums[:, 0:2, :], in0=sums[:, 0:2, :], in1=sums[:, 2:4, :], op=ADD)
+        nc.vector.tensor_tensor(out=sums[:, 0, :], in0=sums[:, 0, :], in1=sums[:, 1, :], op=ADD)
+        means = keep.tile([P, 2, 4, P], BF16)
+        nc.scalar.activation(
+            out=means[:],
+            in_=sums[:, 0, :].rearrange("q (g p t) -> q g t p", g=2, t=4),
+            func=ACT.Copy,
+            scale=1.0 / RANKS,
+        )
+        spins_grouped = keep.tile([P, 2, 2, P, 4], BF16, align_bytes=64)
+        own = psum_flip.tile([P, 2, 4, P], BF16, tag="flip")
+        other = psum_flip.tile([P, 2, 4, P], BF16, tag="flip")
+        for g in range(2):
+            for t in range(4):
+                nc.tensor.transpose(own[:, g, t, :], means[:, g, t, :], ident_bf[:])
+        for g in range(2):
+            for t in range(4):
+                nc.tensor.transpose(other[:, g, t, :], means[:, g, t, :], swap[:])
+        nc.vector.tensor_copy(out=spins_grouped[:, 0], in_=own[:].rearrange("p g t q -> p g q t"))
+        nc.scalar.copy(out=spins_grouped[:, 1], in_=other[:].rearrange("p g t q -> p g q t"))
+        spins_codes = keep.tile([P, 4, P], U32, align_bytes=64)
+        spins_scales = keep.tile([P, 4, P], U8, align_bytes=64)
+        nc.vector.quantize_mx(
+            out=spins_codes[:].rearrange("p g q -> p (g q)").bitcast(FP8X4),
+            scales=spins_scales[:].rearrange("p g q -> p (g q)"),
+            in_=spins_grouped[:].rearrange("p v g q t -> p (v g q t)"),
+        )
+        for half in range(HALVES):
+            cols = slice(N_HALF * half, N_HALF * (half + 1))
+            bias_acc = psum_acc.tile([P, N_HALF], F32, tag="acc")
+            nc.tensor.matmul(out=bias_acc[:], lhsT=ones[:], rhs=bias_row[:, cols], start=True, stop=True)
+            nc.scalar.copy(out=mixed[:, cols], in_=bias_acc[:])
+        for half in range(HALVES):
+            cols = slice(N_HALF * half, N_HALF * (half + 1))
+            acc = psum_acc.tile([P, N_HALF], F32, tag="acc")
+            for g in range(4):
+                mx_pass(acc[:], spins_codes[:, g, :], spins_scales[:, g, :], PASS_MIXED + g, half, g == 0, g == 3)
+            nc.vector.tensor_tensor(out=mixed[:, cols], in0=acc[:], in1=mixed[:, cols], op=ADD)
+
+        for s in range(1, RANKS + 2):
+            if s < RANKS:
+                average_pairs(s)
+            if s - 1 < RANKS:
+                tokens_to_partitions(s - 1)
+            if s - 2 >= 0:
+                finish(s - 2)
+            if s - 1 < RANKS:
+                quantise_pairs(s - 1)

@@ -126,15 +126,16 @@ def tile_ferminetoneelectronlayer_pa_kernel(
         for r in range(0, RANKS, 2):
             nc.sync.dma_start(out=x1[:, r : r + 2, :], in_=x1_rows[:, r : r + 2, :])
         load_pairs(0)
+        load_pairs(1)
         load_scales(PASS_MIXED, w_mixed_scales)
         load_scales(PASS_UNMIXED, w_unmixed_scales)
         load_scales(PASS_2E, w_2e_scales)
         nc.sync.dma_start(out=bias_row[0:1, :], in_=b_unmixed.unsqueeze(0))
         load_words(PASS_MIXED, w_mixed_words)
-        load_pairs(1)
+        load_pairs(2)
         load_words(PASS_UNMIXED, w_unmixed_words)
         load_words(PASS_2E, w_2e_words)
-        for r in range(2, RANKS):
+        for r in range(3, RANKS):
             load_pairs(r)
 
         def mx_pass(acc, codes, scales, w_pass, half, start, stop):
@@ -255,53 +256,64 @@ def tile_ferminetoneelectronlayer_pa_kernel(
                 nc.gpsimd.tensor_tensor(out=result[:, cols], in0=totals[half][:], in1=x1[:, r, cols], op=ADD)
             nc.sync.dma_start(out=out_rows[:, r, :], in_=result[:])
 
-        average_pairs(0)
-
-        nc.vector.tensor_tensor(out=sums[:, 0:2, :], in0=sums[:, 0:2, :], in1=sums[:, 2:4, :], op=ADD)
-        nc.vector.tensor_tensor(out=sums[:, 0, :], in0=sums[:, 0, :], in1=sums[:, 1, :], op=ADD)
-        means = keep.tile([P, 2, 4, P], BF16)
-        nc.scalar.activation(
-            out=means[:],
-            in_=sums[:, 0, :].rearrange("q (g p t) -> q g t p", g=2, t=4),
-            func=ACT.Copy,
-            scale=1.0 / RANKS,
-        )
-        spins_grouped = keep.tile([P, 2, 2, P, 4], BF16, align_bytes=64)
-        own = psum_flip.tile([P, 2, 4, P], BF16, tag="flip")
-        other = psum_flip.tile([P, 2, 4, P], BF16, tag="flip")
-        for g in range(2):
-            for t in range(4):
-                nc.tensor.transpose(own[:, g, t, :], means[:, g, t, :], ident_bf[:])
-        for g in range(2):
-            for t in range(4):
-                nc.tensor.transpose(other[:, g, t, :], means[:, g, t, :], swap[:])
-        nc.vector.tensor_copy(out=spins_grouped[:, 0], in_=own[:].rearrange("p g t q -> p g q t"))
-        nc.scalar.copy(out=spins_grouped[:, 1], in_=other[:].rearrange("p g t q -> p g q t"))
         spins_codes = keep.tile([P, 4, P], U32, align_bytes=64)
         spins_scales = keep.tile([P, 4, P], U8, align_bytes=64)
-        nc.vector.quantize_mx(
-            out=spins_codes[:].rearrange("p g q -> p (g q)").bitcast(FP8X4),
-            scales=spins_scales[:].rearrange("p g q -> p (g q)"),
-            in_=spins_grouped[:].rearrange("p v g q t -> p (v g q t)"),
-        )
-        for half in range(HALVES):
-            cols = slice(N_HALF * half, N_HALF * (half + 1))
-            bias_acc = psum_acc.tile([P, N_HALF], F32, tag="acc")
-            nc.tensor.matmul(out=bias_acc[:], lhsT=ones[:], rhs=bias_row[:, cols], start=True, stop=True)
-            nc.scalar.copy(out=mixed[:, cols], in_=bias_acc[:])
-        for half in range(HALVES):
-            cols = slice(N_HALF * half, N_HALF * (half + 1))
-            acc = psum_acc.tile([P, N_HALF], F32, tag="acc")
-            for g in range(4):
-                mx_pass(acc[:], spins_codes[:, g, :], spins_scales[:, g, :], PASS_MIXED + g, half, g == 0, g == 3)
-            nc.vector.tensor_tensor(out=mixed[:, cols], in0=acc[:], in1=mixed[:, cols], op=ADD)
+        means = keep.tile([P, 2, 4, P], BF16)
 
-        for s in range(1, RANKS + 2):
+        def average_spins():
+            nc.vector.tensor_tensor(out=sums[:, 0:2, :], in0=sums[:, 0:2, :], in1=sums[:, 2:4, :], op=ADD)
+            nc.vector.tensor_tensor(out=sums[:, 0, :], in0=sums[:, 0, :], in1=sums[:, 1, :], op=ADD)
+            nc.scalar.activation(
+                out=means[:],
+                in_=sums[:, 0, :].rearrange("q (g p t) -> q g t p", g=2, t=4),
+                func=ACT.Copy,
+                scale=1.0 / RANKS,
+            )
+
+        def quantise_spins():
+            spins_grouped = keep.tile([P, 2, 2, P, 4], BF16, align_bytes=64)
+            own = psum_flip.tile([P, 2, 4, P], BF16, tag="flip")
+            other = psum_flip.tile([P, 2, 4, P], BF16, tag="flip")
+            for g in range(2):
+                for t in range(4):
+                    nc.tensor.transpose(own[:, g, t, :], means[:, g, t, :], ident_bf[:])
+            for g in range(2):
+                for t in range(4):
+                    nc.tensor.transpose(other[:, g, t, :], means[:, g, t, :], swap[:])
+            nc.vector.tensor_copy(out=spins_grouped[:, 0], in_=own[:].rearrange("p g t q -> p g q t"))
+            nc.scalar.copy(out=spins_grouped[:, 1], in_=other[:].rearrange("p g t q -> p g q t"))
+            nc.vector.quantize_mx(
+                out=spins_codes[:].rearrange("p g q -> p (g q)").bitcast(FP8X4),
+                scales=spins_scales[:].rearrange("p g q -> p (g q)"),
+                in_=spins_grouped[:].rearrange("p v g q t -> p (v g q t)"),
+            )
+
+        def mixed_term():
+            for half in range(HALVES):
+                cols = slice(N_HALF * half, N_HALF * (half + 1))
+                bias_acc = psum_acc.tile([P, N_HALF], F32, tag="acc")
+                nc.tensor.matmul(out=bias_acc[:], lhsT=ones[:], rhs=bias_row[:, cols], start=True, stop=True)
+                nc.scalar.copy(out=mixed[:, cols], in_=bias_acc[:])
+            for half in range(HALVES):
+                cols = slice(N_HALF * half, N_HALF * (half + 1))
+                acc = psum_acc.tile([P, N_HALF], F32, tag="acc")
+                for g in range(4):
+                    mx_pass(acc[:], spins_codes[:, g, :], spins_scales[:, g, :], PASS_MIXED + g, half, g == 0, g == 3)
+                nc.vector.tensor_tensor(out=mixed[:, cols], in0=acc[:], in1=mixed[:, cols], op=ADD)
+
+        average_spins()
+        for s in range(RANKS + 2):
             if s < RANKS:
                 average_pairs(s)
-            if s - 1 < RANKS:
+            if 1 <= s <= RANKS:
                 tokens_to_partitions(s - 1)
-            if s - 2 >= 0:
+            if s == 1:
+                quantise_spins()
+            if s == 2:
+                mixed_term()
+            if s == 3:
+                finish(0)
+            if s >= 3:
                 finish(s - 2)
-            if s - 1 < RANKS:
+            if 1 <= s <= RANKS:
                 quantise_pairs(s - 1)

@@ -123,13 +123,13 @@ def tile_ferminetoneelectronlayer_pa_kernel(
                 )
             pair_tiles.append(pairs)
 
+        load_scales(PASS_MIXED, w_mixed_scales)
+        load_scales(PASS_UNMIXED, w_unmixed_scales)
+        load_scales(PASS_2E, w_2e_scales)
         for r in range(0, RANKS, 2):
             nc.sync.dma_start(out=x1[:, r : r + 2, :], in_=x1_rows[:, r : r + 2, :])
         load_pairs(0)
         load_pairs(1)
-        load_scales(PASS_MIXED, w_mixed_scales)
-        load_scales(PASS_UNMIXED, w_unmixed_scales)
-        load_scales(PASS_2E, w_2e_scales)
         nc.sync.dma_start(out=bias_row[0:1, :], in_=b_unmixed.unsqueeze(0))
         load_words(PASS_MIXED, w_mixed_words)
         load_pairs(2)

@@ -24,6 +24,7 @@ HALVES = D1 // N_HALF
 K_PASS = 512
 GROUPS = 8
 GROUP_TOKENS = P // GROUPS
+FINISH_LAG = 3
 
 PASS_UNMIXED = 0
 PASS_MIXED = 2
@@ -53,32 +54,33 @@ def tile_ferminetoneelectronlayer_pa_kernel(
         pair_pool = ctx.enter_context(tc.tile_pool(name="pair_pool", bufs=RANKS))
         out_pool = ctx.enter_context(tc.tile_pool(name="out_pool", bufs=RANKS))
         work = ctx.enter_context(tc.tile_pool(name="work", bufs=2))
+        totals_pool = ctx.enter_context(tc.tile_pool(name="totals_pool", bufs=4))
         psum_sums = ctx.enter_context(tc.psum_pool(name="psum_sums", bufs=2))
         psum_flip = ctx.enter_context(tc.psum_pool(name="psum_flip", bufs=3))
         psum_acc = ctx.enter_context(tc.psum_pool(name="psum_acc", bufs=3))
-        totals_pool = ctx.enter_context(tc.tile_pool(name="totals_pool", bufs=4))
         ctx.enter_context(tc.manual_schedule())
 
         x1_rows = in_1e.flatten_outer_dims().rearrange("(q r) k -> q r k", r=RANKS)
         out_rows = out.flatten_outer_dims().rearrange("(q r) n -> q r n", r=RANKS)
         pair_rows = in_2e.rearrange("b (s r) (c j a) d -> (b s) r (c j) (a d)", s=SPINS, c=SPINS, a=2)
 
-        w_scales = keep.tile([P, PASSES, D1], U8, align_bytes=64)
-        nc.vector.memset(w_scales[:].bitcast(I32), 0)
-        bias_row = keep.tile([P, D1], BF16)
-        nc.vector.memset(bias_row[:], 0.0)
-        ident_bf = const.tile([P, P], BF16)
-        make_identity(nc, ident_bf[:])
         ident_f32 = const.tile([P, P], F32)
         make_identity(nc, ident_f32[:])
+        ident_bf = const.tile([P, P], BF16)
+        make_identity(nc, ident_bf[:])
+        bias_row = keep.tile([P, D1], BF16)
+        nc.gpsimd.memset(bias_row[:], 0.0)
+        nc.gpsimd.dma_start(out=bias_row[0:1, :], in_=b_unmixed.unsqueeze(0))
+        w_scales = keep.tile([P, PASSES, D1], U8, align_bytes=64)
+        nc.gpsimd.memset(w_scales[:].bitcast(F32), 0.0)
+        ones = const.tile([P, P], BF16)
+        nc.gpsimd.memset(ones[:], 1.0)
         swap = const.tile([P, P], BF16)
         for s in range(SPINS):
             nc.vector.tensor_copy(
                 out=swap[:].rearrange("p (b s) -> p b s", s=SPINS)[:, :, s],
                 in_=ident_bf[:].rearrange("p (b s) -> p b s", s=SPINS)[:, :, 1 - s],
             )
-        ones = const.tile([P, P], BF16)
-        nc.vector.memset(ones[:], 1.0)
         member = const.tile([P, 2 * GROUP_TOKENS], F32)
         nc.vector.tensor_reduce(
             out=member[:],
@@ -123,14 +125,13 @@ def tile_ferminetoneelectronlayer_pa_kernel(
                 )
             pair_tiles.append(pairs)
 
-        load_scales(PASS_MIXED, w_mixed_scales)
-        load_scales(PASS_UNMIXED, w_unmixed_scales)
-        load_scales(PASS_2E, w_2e_scales)
         for r in range(0, RANKS, 2):
             nc.sync.dma_start(out=x1[:, r : r + 2, :], in_=x1_rows[:, r : r + 2, :])
         load_pairs(0)
         load_pairs(1)
-        nc.sync.dma_start(out=bias_row[0:1, :], in_=b_unmixed.unsqueeze(0))
+        load_scales(PASS_MIXED, w_mixed_scales)
+        load_scales(PASS_UNMIXED, w_unmixed_scales)
+        load_scales(PASS_2E, w_2e_scales)
         load_words(PASS_MIXED, w_mixed_words)
         load_pairs(2)
         load_words(PASS_UNMIXED, w_unmixed_words)
@@ -149,11 +150,10 @@ def tile_ferminetoneelectronlayer_pa_kernel(
                 stop=stop,
             )
 
+        x1_grouped = keep.tile([P, RANKS, 2 * K_PASS], BF16, align_bytes=64)
         x1_codes = keep.tile([P, RANKS, 2 * P], U32, align_bytes=64)
         x1_scales = keep.tile([P, RANKS, 2 * P], U8, align_bytes=64)
-        sums = keep.tile([P, 4, D1], F32)
-
-        def flip_x1(r):
+        for r in range(RANKS):
             x1_words = x1[:, r, :].bitcast(F32)
             flipped = psum_flip.tile([P, 2, 2, P], F32, tag="flip")
             for g in range(2):
@@ -163,26 +163,81 @@ def tile_ferminetoneelectronlayer_pa_kernel(
                         x1_words[:, 256 * g + u : 256 * (g + 1) : 2],
                         ident_f32[:],
                     )
-            x1_grouped = work.tile([P, 2 * K_PASS], BF16, align_bytes=64)
             nc.scalar.copy(
-                out=x1_grouped[:].bitcast(F32).rearrange("p (g q u) -> p g q u", g=2, u=2),
+                out=x1_grouped[:, r, :].bitcast(F32).rearrange("p (g q u) -> p g q u", g=2, u=2),
                 in_=flipped[:].rearrange("p g u q -> p g q u"),
             )
-            return x1_grouped
 
-        for c in range(4):
-            grouped_pair = [flip_x1(2 * c), flip_x1(2 * c + 1)]
-            nc.vector.tensor_tensor(out=sums[:, c, :], in0=x1[:, 2 * c, :], in1=x1[:, 2 * c + 1, :], op=ADD)
-            for i in range(2):
+        def quantise_x1():
+            for r in range(0, RANKS, 4):
                 nc.vector.quantize_mx(
-                    out=x1_codes[:, 2 * c + i, :].bitcast(FP8X4),
-                    scales=x1_scales[:, 2 * c + i, :],
-                    in_=grouped_pair[i][:],
+                    out=x1_codes[:, r : r + 4, :].rearrange("p r q -> p (r q)").bitcast(FP8X4),
+                    scales=x1_scales[:, r : r + 4, :].rearrange("p r q -> p (r q)"),
+                    in_=x1_grouped[:, r : r + 4, :].rearrange("p r k -> p (r k)"),
                 )
+
+        running = keep.tile([P, D1], F32)
+        spin_sums = keep.tile([P, 2, 4, P], BF16)
+        nc.vector.tensor_tensor(out=running[:], in0=x1[:, 0, :], in1=x1[:, 1, :], op=ADD)
+        for r in range(2, RANKS, 2):
+            two_rows = work.tile([P, D1], F32)
+            nc.vector.tensor_tensor(out=two_rows[:], in0=x1[:, r, :], in1=x1[:, r + 1, :], op=ADD)
+            if r + 2 < RANKS:
+                nc.vector.tensor_tensor(out=running[:], in0=running[:], in1=two_rows[:], op=ADD)
+            else:
+                nc.vector.tensor_tensor(
+                    out=spin_sums[:],
+                    in0=running[:].rearrange("q (g p t) -> q g t p", g=2, t=4),
+                    in1=two_rows[:].rearrange("q (g p t) -> q g t p", g=2, t=4),
+                    op=ADD,
+                )
+
+        spins_codes = keep.tile([P, 4, P], U32, align_bytes=64)
+        spins_scales = keep.tile([P, 4, P], U8, align_bytes=64)
+        mixed = keep.tile([P, D1], F32)
+
+        def quantise_spins():
+            spins_grouped = keep.tile([P, 2, 2, P, 4], BF16, align_bytes=64)
+            own = psum_flip.tile([P, 2, 4, P], BF16, tag="flip")
+            other = psum_flip.tile([P, 2, 4, P], BF16, tag="flip")
+            for g in range(2):
+                for t in range(4):
+                    nc.tensor.transpose(own[:, g, t, :], spin_sums[:, g, t, :], ident_bf[:])
+            for g in range(2):
+                for t in range(4):
+                    nc.tensor.transpose(other[:, g, t, :], spin_sums[:, g, t, :], swap[:])
+            nc.vector.tensor_scalar_mul(
+                out=spins_grouped[:, 0], in0=own[:].rearrange("p g t q -> p g q t"), scalar1=1.0 / RANKS
+            )
+            nc.scalar.activation(
+                out=spins_grouped[:, 1],
+                in_=other[:].rearrange("p g t q -> p g q t"),
+                func=ACT.Copy,
+                scale=1.0 / RANKS,
+            )
+            nc.vector.quantize_mx(
+                out=spins_codes[:].rearrange("p g q -> p (g q)").bitcast(FP8X4),
+                scales=spins_scales[:].rearrange("p g q -> p (g q)"),
+                in_=spins_grouped[:].rearrange("p v g q t -> p (v g q t)"),
+            )
+
+        def spread_bias():
+            for half in range(HALVES):
+                cols = slice(N_HALF * half, N_HALF * (half + 1))
+                bias_acc = psum_acc.tile([P, N_HALF], F32, tag="acc")
+                nc.tensor.matmul(out=bias_acc[:], lhsT=ones[:], rhs=bias_row[:, cols], start=True, stop=True)
+                nc.scalar.copy(out=mixed[:, cols], in_=bias_acc[:])
+
+        def mixed_term():
+            for half in range(HALVES):
+                cols = slice(N_HALF * half, N_HALF * (half + 1))
+                acc = psum_acc.tile([P, N_HALF], F32, tag="acc")
+                for g in range(4):
+                    mx_pass(acc[:], spins_codes[:, g, :], spins_scales[:, g, :], PASS_MIXED + g, half, g == 0, g == 3)
+                nc.vector.tensor_tensor(out=mixed[:, cols], in0=acc[:], in1=mixed[:, cols], op=ADD)
 
         pair_codes = keep.tile([P, RANKS, P], U32, align_bytes=64)
         pair_scales = keep.tile([P, RANKS, P], U8, align_bytes=64)
-        mixed = keep.tile([P, D1], F32)
         pair_means_of = {}
         sorted_k_of = {}
 
@@ -254,66 +309,20 @@ def tile_ferminetoneelectronlayer_pa_kernel(
             for half in range(HALVES):
                 cols = slice(N_HALF * half, N_HALF * (half + 1))
                 nc.gpsimd.tensor_tensor(out=result[:, cols], in0=totals[half][:], in1=x1[:, r, cols], op=ADD)
-            nc.sync.dma_start(out=out_rows[:, r, :], in_=result[:])
+                nc.sync.dma_start(out=out_rows[:, r, cols], in_=result[:, cols])
 
-        spins_codes = keep.tile([P, 4, P], U32, align_bytes=64)
-        spins_scales = keep.tile([P, 4, P], U8, align_bytes=64)
-        means = keep.tile([P, 2, 4, P], BF16)
-
-        def average_spins():
-            nc.vector.tensor_tensor(out=sums[:, 0:2, :], in0=sums[:, 0:2, :], in1=sums[:, 2:4, :], op=ADD)
-            nc.vector.tensor_tensor(out=sums[:, 0, :], in0=sums[:, 0, :], in1=sums[:, 1, :], op=ADD)
-            nc.scalar.activation(
-                out=means[:],
-                in_=sums[:, 0, :].rearrange("q (g p t) -> q g t p", g=2, t=4),
-                func=ACT.Copy,
-                scale=1.0 / RANKS,
-            )
-
-        def quantise_spins():
-            spins_grouped = keep.tile([P, 2, 2, P, 4], BF16, align_bytes=64)
-            own = psum_flip.tile([P, 2, 4, P], BF16, tag="flip")
-            other = psum_flip.tile([P, 2, 4, P], BF16, tag="flip")
-            for g in range(2):
-                for t in range(4):
-                    nc.tensor.transpose(own[:, g, t, :], means[:, g, t, :], ident_bf[:])
-            for g in range(2):
-                for t in range(4):
-                    nc.tensor.transpose(other[:, g, t, :], means[:, g, t, :], swap[:])
-            nc.vector.tensor_copy(out=spins_grouped[:, 0], in_=own[:].rearrange("p g t q -> p g q t"))
-            nc.scalar.copy(out=spins_grouped[:, 1], in_=other[:].rearrange("p g t q -> p g q t"))
-            nc.vector.quantize_mx(
-                out=spins_codes[:].rearrange("p g q -> p (g q)").bitcast(FP8X4),
-                scales=spins_scales[:].rearrange("p g q -> p (g q)"),
-                in_=spins_grouped[:].rearrange("p v g q t -> p (v g q t)"),
-            )
-
-        def mixed_term():
-            for half in range(HALVES):
-                cols = slice(N_HALF * half, N_HALF * (half + 1))
-                bias_acc = psum_acc.tile([P, N_HALF], F32, tag="acc")
-                nc.tensor.matmul(out=bias_acc[:], lhsT=ones[:], rhs=bias_row[:, cols], start=True, stop=True)
-                nc.scalar.copy(out=mixed[:, cols], in_=bias_acc[:])
-            for half in range(HALVES):
-                cols = slice(N_HALF * half, N_HALF * (half + 1))
-                acc = psum_acc.tile([P, N_HALF], F32, tag="acc")
-                for g in range(4):
-                    mx_pass(acc[:], spins_codes[:, g, :], spins_scales[:, g, :], PASS_MIXED + g, half, g == 0, g == 3)
-                nc.vector.tensor_tensor(out=mixed[:, cols], in0=acc[:], in1=mixed[:, cols], op=ADD)
-
-        average_spins()
-        for s in range(RANKS + 2):
-            if s < RANKS:
-                average_pairs(s)
+        for s in range(RANKS + FINISH_LAG):
             if 1 <= s <= RANKS:
                 tokens_to_partitions(s - 1)
-            if s == 1:
-                quantise_spins()
             if s == 2:
                 mixed_term()
-            if s == 3:
-                finish(0)
-            if s >= 3:
-                finish(s - 2)
+            if s < RANKS:
+                average_pairs(s)
+            if s == 1:
+                quantise_spins()
+                spread_bias()
+                quantise_x1()
+            if s >= FINISH_LAG:
+                finish(s - FINISH_LAG)
             if 1 <= s <= RANKS:
                 quantise_pairs(s - 1)

@@ -116,10 +116,10 @@ def tile_ferminetoneelectronlayer_pa_kernel(
                 in_=words.rearrange("g p n -> p g n").bitcast(I32),
             )
 
-        def load_pairs(r):
+        def load_pairs(r, queue):
             pairs = pair_pool.tile([P, GROUPS, 2 * D2], BF16)
             for grp in range(GROUPS):
-                nc.sync.dma_start(
+                queue.dma_start(
                     out=pairs[:, grp, :],
                     in_=pair_rows[GROUP_TOKENS * grp : GROUP_TOKENS * (grp + 1), r],
                 )
@@ -127,17 +127,17 @@ def tile_ferminetoneelectronlayer_pa_kernel(
 
         for r in range(0, RANKS, 2):
             nc.sync.dma_start(out=x1[:, r : r + 2, :], in_=x1_rows[:, r : r + 2, :])
-        load_pairs(0)
-        load_pairs(1)
+        load_pairs(0, nc.sync)
+        load_pairs(1, nc.sync)
+        load_pairs(2, nc.gpsimd)
         load_scales(PASS_MIXED, w_mixed_scales)
         load_scales(PASS_UNMIXED, w_unmixed_scales)
         load_scales(PASS_2E, w_2e_scales)
         load_words(PASS_MIXED, w_mixed_words)
-        load_pairs(2)
         load_words(PASS_UNMIXED, w_unmixed_words)
         load_words(PASS_2E, w_2e_words)
         for r in range(3, RANKS):
-            load_pairs(r)
+            load_pairs(r, nc.sync)
 
         def mx_pass(acc, codes, scales, w_pass, half, start, stop):
             nc.tensor.matmul_mx(
@@ -306,9 +306,10 @@ def tile_ferminetoneelectronlayer_pa_kernel(
                 )
                 nc.scalar.activation(out=total[:], in_=total[:], func=ACT.Tanh)
                 totals.append(total)
+            adder = nc.vector if r == RANKS - 1 else nc.gpsimd
             for half in range(HALVES):
                 cols = slice(N_HALF * half, N_HALF * (half + 1))
-                nc.gpsimd.tensor_tensor(out=result[:, cols], in0=totals[half][:], in1=x1[:, r, cols], op=ADD)
+                adder.tensor_tensor(out=result[:, cols], in0=totals[half][:], in1=x1[:, r, cols], op=ADD)
                 nc.sync.dma_start(out=out_rows[:, r, cols], in_=result[:, cols])
 
         for s in range(RANKS + FINISH_LAG):

@@ -22,9 +22,10 @@ D2 = 256
 N_HALF = 512
 HALVES = D1 // N_HALF
 K_PASS = 512
-GROUPS = 8
-GROUP_TOKENS = P // GROUPS
-FINISH_LAG = 3
+GROUPS = 2
+GROUP_WALKERS = WALKERS // GROUPS
+ROWS = 2
+PACK = 4
 
 PASS_UNMIXED = 0
 PASS_MIXED = 2
@@ -56,46 +57,32 @@ def tile_ferminetoneelectronlayer_pa_kernel(
         work = ctx.enter_context(tc.tile_pool(name="work", bufs=2))
         totals_pool = ctx.enter_context(tc.tile_pool(name="totals_pool", bufs=4))
         psum_sums = ctx.enter_context(tc.psum_pool(name="psum_sums", bufs=2))
-        psum_flip = ctx.enter_context(tc.psum_pool(name="psum_flip", bufs=3))
-        psum_acc = ctx.enter_context(tc.psum_pool(name="psum_acc", bufs=3))
+        psum_flip = ctx.enter_context(tc.psum_pool(name="psum_flip", bufs=2))
+        psum_acc = ctx.enter_context(tc.psum_pool(name="psum_acc", bufs=4))
         ctx.enter_context(tc.manual_schedule())
 
         x1_rows = in_1e.flatten_outer_dims().rearrange("(q r) k -> q r k", r=RANKS)
         out_rows = out.flatten_outer_dims().rearrange("(q r) n -> q r n", r=RANKS)
-        pair_rows = in_2e.rearrange("b (s r) (c j a) d -> (b s) r (c j) (a d)", s=SPINS, c=SPINS, a=2)
+        pair_rows = in_2e.rearrange("b (s r) (c j a) d -> b s r c j a d", s=SPINS, c=SPINS, a=ROWS)
 
+        w_scales = keep.tile([P, PASSES, D1], U8, align_bytes=64)
+        nc.vector.memset(w_scales[:].bitcast(I32), 0)
         ident_f32 = const.tile([P, P], F32)
         make_identity(nc, ident_f32[:])
-        ident_bf = const.tile([P, P], BF16)
-        make_identity(nc, ident_bf[:])
         bias_row = keep.tile([P, D1], BF16)
         nc.gpsimd.memset(bias_row[:], 0.0)
         nc.gpsimd.dma_start(out=bias_row[0:1, :], in_=b_unmixed.unsqueeze(0))
-        w_scales = keep.tile([P, PASSES, D1], U8, align_bytes=64)
-        nc.gpsimd.memset(w_scales[:].bitcast(F32), 0.0)
         ones = const.tile([P, P], BF16)
         nc.gpsimd.memset(ones[:], 1.0)
-        swap = const.tile([P, P], BF16)
-        for s in range(SPINS):
-            nc.vector.tensor_copy(
-                out=swap[:].rearrange("p (b s) -> p b s", s=SPINS)[:, :, s],
-                in_=ident_bf[:].rearrange("p (b s) -> p b s", s=SPINS)[:, :, 1 - s],
-            )
-        member = const.tile([P, 2 * GROUP_TOKENS], F32)
+        member = const.tile([P, GROUP_WALKERS], F32)
         nc.vector.tensor_reduce(
             out=member[:],
-            in_=ident_bf[:].rearrange("p (g j) -> p g j", j=4),
+            in_=ident_f32[:].rearrange("p (b j) -> p b j", b=GROUP_WALKERS),
             axis=mybir.AxisListType.X,
             op=ADD,
         )
-        averager = const.tile([P, SPINS, GROUP_TOKENS], BF16)
-        for s in range(SPINS):
-            for o in range(SPINS):
-                nc.vector.tensor_scalar_mul(
-                    out=averager[:].rearrange("p o (b s) -> p o b s", s=SPINS)[:, o, :, s],
-                    in0=member[:].rearrange("p (b s c) -> p b s c", s=SPINS, c=SPINS)[:, :, s, (o + s) % SPINS],
-                    scalar1=1.0 / RANKS,
-                )
+        averager = const.tile([P, GROUP_WALKERS], BF16)
+        nc.vector.tensor_scalar_mul(out=averager[:], in0=member[:], scalar1=1.0 / RANKS)
 
         w_words = keep.tile([P, PASSES, 2 * D1], U8, align_bytes=64)
         x1 = keep.tile([P, RANKS, D1], BF16)
@@ -117,26 +104,26 @@ def tile_ferminetoneelectronlayer_pa_kernel(
             )
 
         def load_pairs(r, queue):
-            pairs = pair_pool.tile([P, GROUPS, 2 * D2], BF16)
-            for grp in range(GROUPS):
-                queue.dma_start(
-                    out=pairs[:, grp, :],
-                    in_=pair_rows[GROUP_TOKENS * grp : GROUP_TOKENS * (grp + 1), r],
-                )
+            pairs = pair_pool.tile([P, SPINS, GROUPS, ROWS, SPINS, D2], BF16)
+            for s in range(SPINS):
+                for grp in range(GROUPS):
+                    for o in range(SPINS):
+                        queue.dma_start(
+                            out=pairs[:, s, grp, :, o, :],
+                            in_=pair_rows[GROUP_WALKERS * grp : GROUP_WALKERS * (grp + 1), s, r, (s + o) % SPINS],
+                        )
             pair_tiles.append(pairs)
 
         for r in range(0, RANKS, 2):
             nc.sync.dma_start(out=x1[:, r : r + 2, :], in_=x1_rows[:, r : r + 2, :])
-        load_pairs(0, nc.sync)
-        load_pairs(1, nc.sync)
-        load_pairs(2, nc.gpsimd)
-        load_scales(PASS_MIXED, w_mixed_scales)
-        load_scales(PASS_UNMIXED, w_unmixed_scales)
-        load_scales(PASS_2E, w_2e_scales)
-        load_words(PASS_MIXED, w_mixed_words)
         load_words(PASS_UNMIXED, w_unmixed_words)
+        load_scales(PASS_UNMIXED, w_unmixed_scales)
+        load_scales(PASS_MIXED, w_mixed_scales)
+        load_scales(PASS_2E, w_2e_scales)
+        load_pairs(0, nc.sync)
+        load_words(PASS_MIXED, w_mixed_words)
         load_words(PASS_2E, w_2e_words)
-        for r in range(3, RANKS):
+        for r in range(1, RANKS):
             load_pairs(r, nc.sync)
 
         def mx_pass(acc, codes, scales, w_pass, half, start, stop):
@@ -155,7 +142,10 @@ def tile_ferminetoneelectronlayer_pa_kernel(
         x1_scales = keep.tile([P, RANKS, 2 * P], U8, align_bytes=64)
         for r in range(RANKS):
             x1_words = x1[:, r, :].bitcast(F32)
-            flipped = psum_flip.tile([P, 2, 2, P], F32, tag="flip")
+            if r % 2 == 0:
+                flipped = psum_flip.tile([P, 2, 2, P], F32, tag="flip")
+            else:
+                flipped = psum_acc.tile([P, 2, 2, P], F32, tag="acc")
             for g in range(2):
                 for u in range(2):
                     nc.tensor.transpose(
@@ -168,125 +158,114 @@ def tile_ferminetoneelectronlayer_pa_kernel(
                 in_=flipped[:].rearrange("p g u q -> p g q u"),
             )
 
-        def quantise_x1():
-            for r in range(0, RANKS, 4):
-                nc.vector.quantize_mx(
-                    out=x1_codes[:, r : r + 4, :].rearrange("p r q -> p (r q)").bitcast(FP8X4),
-                    scales=x1_scales[:, r : r + 4, :].rearrange("p r q -> p (r q)"),
-                    in_=x1_grouped[:, r : r + 4, :].rearrange("p r k -> p (r k)"),
-                )
+        def quantise_x1(r, tiles):
+            nc.vector.quantize_mx(
+                out=x1_codes[:, r : r + tiles, :].rearrange("p r q -> p (r q)").bitcast(FP8X4),
+                scales=x1_scales[:, r : r + tiles, :].rearrange("p r q -> p (r q)"),
+                in_=x1_grouped[:, r : r + tiles, :].rearrange("p r k -> p (r k)"),
+            )
 
         running = keep.tile([P, D1], F32)
-        spin_sums = keep.tile([P, 2, 4, P], BF16)
-        nc.vector.tensor_tensor(out=running[:], in0=x1[:, 0, :], in1=x1[:, 1, :], op=ADD)
-        for r in range(2, RANKS, 2):
-            two_rows = work.tile([P, D1], F32)
-            nc.vector.tensor_tensor(out=two_rows[:], in0=x1[:, r, :], in1=x1[:, r + 1, :], op=ADD)
-            if r + 2 < RANKS:
-                nc.vector.tensor_tensor(out=running[:], in0=running[:], in1=two_rows[:], op=ADD)
-            else:
-                nc.vector.tensor_tensor(
-                    out=spin_sums[:],
-                    in0=running[:].rearrange("q (g p t) -> q g t p", g=2, t=4),
-                    in1=two_rows[:].rearrange("q (g p t) -> q g t p", g=2, t=4),
-                    op=ADD,
-                )
-
-        spins_codes = keep.tile([P, 4, P], U32, align_bytes=64)
-        spins_scales = keep.tile([P, 4, P], U8, align_bytes=64)
+        spins_grouped = keep.tile([P, SPINS, 2, P, PACK], BF16, align_bytes=64)
+        spins_codes = keep.tile([P, SPINS, 2 * P], U32, align_bytes=64)
+        spins_scales = keep.tile([P, SPINS, 2 * P], U8, align_bytes=64)
         mixed = keep.tile([P, D1], F32)
 
+        def sum_spins():
+            own = spins_grouped[:, 0].rearrange("p g q t -> p (g q t)")
+            nc.vector.tensor_tensor(out=running[:], in0=x1_grouped[:, 0, :], in1=x1_grouped[:, 1, :], op=ADD)
+            for r in range(2, RANKS, 2):
+                two_rows = work.tile([P, D1], F32)
+                nc.vector.tensor_tensor(out=two_rows[:], in0=x1_grouped[:, r, :], in1=x1_grouped[:, r + 1, :], op=ADD)
+                total = running[:] if r + 2 < RANKS else own
+                nc.vector.tensor_tensor(out=total, in0=running[:], in1=two_rows[:], op=ADD)
+                if r == 2:
+                    quantise_x1(0, 2)
+
         def quantise_spins():
-            spins_grouped = keep.tile([P, 2, 2, P, 4], BF16, align_bytes=64)
-            own = psum_flip.tile([P, 2, 4, P], BF16, tag="flip")
-            other = psum_flip.tile([P, 2, 4, P], BF16, tag="flip")
-            for g in range(2):
-                for t in range(4):
-                    nc.tensor.transpose(own[:, g, t, :], spin_sums[:, g, t, :], ident_bf[:])
-            for g in range(2):
-                for t in range(4):
-                    nc.tensor.transpose(other[:, g, t, :], spin_sums[:, g, t, :], swap[:])
-            nc.vector.tensor_scalar_mul(
-                out=spins_grouped[:, 0], in0=own[:].rearrange("p g t q -> p g q t"), scalar1=1.0 / RANKS
-            )
-            nc.scalar.activation(
-                out=spins_grouped[:, 1],
-                in_=other[:].rearrange("p g t q -> p g q t"),
-                func=ACT.Copy,
-                scale=1.0 / RANKS,
-            )
-            nc.vector.quantize_mx(
-                out=spins_codes[:].rearrange("p g q -> p (g q)").bitcast(FP8X4),
-                scales=spins_scales[:].rearrange("p g q -> p (g q)"),
-                in_=spins_grouped[:].rearrange("p v g q t -> p (v g q t)"),
-            )
+            for s in range(SPINS):
+                nc.scalar.copy(
+                    out=spins_grouped[:, 1].rearrange("p g (b s) t -> p g b s t", s=SPINS)[:, :, :, s, :],
+                    in_=spins_grouped[:, 0].rearrange("p g (b s) t -> p g b s t", s=SPINS)[:, :, :, 1 - s, :],
+                )
+            for o in range(SPINS):
+                nc.vector.quantize_mx(
+                    out=spins_codes[:, o, :].bitcast(FP8X4),
+                    scales=spins_scales[:, o, :],
+                    in_=spins_grouped[:, o].rearrange("p g q t -> p (g q t)"),
+                )
 
         def spread_bias():
             for half in range(HALVES):
                 cols = slice(N_HALF * half, N_HALF * (half + 1))
-                bias_acc = psum_acc.tile([P, N_HALF], F32, tag="acc")
+                bias_acc = psum_flip.tile([P, N_HALF], F32, tag="flip")
                 nc.tensor.matmul(out=bias_acc[:], lhsT=ones[:], rhs=bias_row[:, cols], start=True, stop=True)
                 nc.scalar.copy(out=mixed[:, cols], in_=bias_acc[:])
 
         def mixed_term():
             for half in range(HALVES):
                 cols = slice(N_HALF * half, N_HALF * (half + 1))
-                acc = psum_acc.tile([P, N_HALF], F32, tag="acc")
-                for g in range(4):
-                    mx_pass(acc[:], spins_codes[:, g, :], spins_scales[:, g, :], PASS_MIXED + g, half, g == 0, g == 3)
-                nc.vector.tensor_tensor(out=mixed[:, cols], in0=acc[:], in1=mixed[:, cols], op=ADD)
+                acc = psum_flip.tile([P, N_HALF], F32, tag="flip")
+                for o in range(SPINS):
+                    for g in range(2):
+                        mx_pass(
+                            acc[:],
+                            spins_codes[:, o, P * g : P * (g + 1)],
+                            spins_scales[:, o, P * g : P * (g + 1)],
+                            PASS_MIXED + 2 * o + g,
+                            half,
+                            o + g == 0,
+                            o + g == 2,
+                        )
+                nc.vector.scalar_tensor_tensor(
+                    out=mixed[:, cols],
+                    in0=acc[:],
+                    scalar=1.0 / RANKS,
+                    in1=mixed[:, cols],
+                    op0=mybir.AluOpType.mult,
+                    op1=ADD,
+                )
 
         pair_codes = keep.tile([P, RANKS, P], U32, align_bytes=64)
         pair_scales = keep.tile([P, RANKS, P], U8, align_bytes=64)
-        pair_means_of = {}
-        sorted_k_of = {}
+        pair_sums_of = {}
 
         def average_pairs(r):
             pairs = pair_tiles[r]
-            pair_sums = psum_sums.tile([P, 2, SPINS, GROUPS, GROUP_TOKENS], F32)
-            for grp in range(GROUPS):
-                for h in range(2):
-                    for a in range(2):
-                        nc.tensor.matmul(
-                            out=pair_sums[:, h, :, grp, :],
-                            lhsT=pairs[:, grp, D2 * a + P * h : D2 * a + P * (h + 1)],
-                            rhs=averager[:],
-                            start=(a == 0),
-                            stop=(a == 1),
-                        )
-            pair_means = work.tile([P, 2, SPINS, P], BF16)
-            nc.scalar.copy(out=pair_means[:], in_=pair_sums[:].rearrange("p h o g q -> p h o (g q)"))
-            pair_means_of[r] = pair_means
+            pair_sums = psum_sums.tile([P, PACK, SPINS, WALKERS], F32)
+            for s in range(SPINS):
+                for grp in range(GROUPS):
+                    for t in range(PACK):
+                        for a in range(ROWS):
+                            row = pairs[:, s, grp, a].rearrange("p o d -> p (o d)")
+                            nc.tensor.matmul(
+                                out=pair_sums[:, t, s, GROUP_WALKERS * grp : GROUP_WALKERS * (grp + 1)],
+                                lhsT=row[:, t : SPINS * D2 : PACK],
+                                rhs=averager[:],
+                                start=(a == 0),
+                                stop=(a == ROWS - 1),
+                            )
+            pair_sums_of[r] = pair_sums
 
-        def tokens_to_partitions(r):
-            pair_means = pair_means_of[r]
-            by_token = psum_flip.tile([P, SPINS, 2, P], BF16, tag="flip")
-            for o in range(SPINS):
-                for h in range(2):
-                    nc.tensor.transpose(by_token[:, o, h, :], pair_means[:, h, o, :], ident_bf[:])
-            sorted_k = work.tile([P, 4, P], BF16)
-            nc.scalar.copy(
-                out=sorted_k[:],
-                in_=by_token[:].rearrange("q o h d -> q (o h d)").rearrange("q (p t) -> q t p", t=4),
-            )
-            sorted_k_of[r] = sorted_k
+        pair_grouped_of = {}
+
+        def group_pairs(r):
+            pair_grouped = work.tile([P, WALKERS, SPINS, PACK], BF16, align_bytes=64)
+            nc.scalar.copy(out=pair_grouped[:], in_=pair_sums_of[r][:].rearrange("p t s b -> p b s t"))
+            pair_grouped_of[r] = pair_grouped
 
         def quantise_pairs(r):
-            sorted_k = sorted_k_of[r]
-            flipped = psum_flip.tile([P, 4, P], BF16, tag="flip")
-            for t in range(4):
-                nc.tensor.transpose(flipped[:, t, :], sorted_k[:, t, :], ident_bf[:])
-            pair_grouped = work.tile([P, P, 4], BF16, align_bytes=64)
-            nc.vector.tensor_copy(out=pair_grouped[:], in_=flipped[:].rearrange("p t q -> p q t"))
             nc.vector.quantize_mx(
                 out=pair_codes[:, r, :].bitcast(FP8X4),
                 scales=pair_scales[:, r, :],
-                in_=pair_grouped[:].rearrange("p q t -> p (q t)"),
+                in_=pair_grouped_of[r][:].rearrange("p b s t -> p (b s t)"),
             )
 
-        def finish(r):
-            result = out_pool.tile([P, D1], F32)
-            totals = []
+        acc_of = {}
+        totals_of = {}
+
+        def start_tile(r):
+            accs = []
             for half in range(HALVES):
                 acc = psum_acc.tile([P, N_HALF], F32, tag="acc")
                 for g in range(2):
@@ -299,31 +278,54 @@ def tile_ferminetoneelectronlayer_pa_kernel(
                         g == 0,
                         False,
                     )
+                accs.append(acc)
+            acc_of[r] = accs
+
+        def add_pairs(r):
+            for half in range(HALVES):
+                acc = acc_of[r][half]
                 mx_pass(acc[:], pair_codes[:, r, :], pair_scales[:, r, :], PASS_2E, half, False, True)
+
+        def add_mixed(r):
+            totals = []
+            for half in range(HALVES):
                 total = totals_pool.tile([P, N_HALF], F32)
                 nc.vector.tensor_tensor(
-                    out=total[:], in0=acc[:], in1=mixed[:, N_HALF * half : N_HALF * (half + 1)], op=ADD
+                    out=total[:], in0=acc_of[r][half][:], in1=mixed[:, N_HALF * half : N_HALF * (half + 1)], op=ADD
                 )
                 nc.scalar.activation(out=total[:], in_=total[:], func=ACT.Tanh)
                 totals.append(total)
+            totals_of[r] = totals
+
+        def add_skip(r):
+            result = out_pool.tile([P, D1], F32)
             adder = nc.vector if r == RANKS - 1 else nc.gpsimd
             for half in range(HALVES):
                 cols = slice(N_HALF * half, N_HALF * (half + 1))
-                adder.tensor_tensor(out=result[:, cols], in0=totals[half][:], in1=x1[:, r, cols], op=ADD)
+                adder.tensor_tensor(out=result[:, cols], in0=totals_of[r][half][:], in1=x1[:, r, cols], op=ADD)
                 nc.sync.dma_start(out=out_rows[:, r, cols], in_=result[:, cols])
 
-        for s in range(RANKS + FINISH_LAG):
-            if 1 <= s <= RANKS:
-                tokens_to_partitions(s - 1)
-            if s == 2:
-                mixed_term()
-            if s < RANKS:
-                average_pairs(s)
-            if s == 1:
-                quantise_spins()
-                spread_bias()
-                quantise_x1()
-            if s >= FINISH_LAG:
-                finish(s - FINISH_LAG)
-            if 1 <= s <= RANKS:
-                quantise_pairs(s - 1)
+        sum_spins()
+        spread_bias()
+        start_tile(0)
+        start_tile(1)
+        average_pairs(0)
+        quantise_spins()
+        quantise_x1(2, 2)
+        group_pairs(0)
+        quantise_pairs(0)
+        quantise_x1(4, 4)
+        mixed_term()
+        average_pairs(1)
+        for r in range(RANKS):
+            add_pairs(r)
+            if r + 2 < RANKS:
+                average_pairs(r + 2)
+            if r + 1 < RANKS:
+                group_pairs(r + 1)
+            add_mixed(r)
+            if r + 1 < RANKS:
+                quantise_pairs(r + 1)
+            add_skip(r)
+            if r + 2 < RANKS:
+                start_tile(r + 2)

@@ -53,7 +53,9 @@ def tile_ferminetoneelectronlayer_pa_kernel(
         const = ctx.enter_context(tc.tile_pool(name="const", bufs=1))
         keep = ctx.enter_context(tc.tile_pool(name="keep", bufs=1))
         pair_pool = ctx.enter_context(tc.tile_pool(name="pair_pool", bufs=RANKS))
+        outer_pool = ctx.enter_context(tc.tile_pool(name="outer_pool", bufs=3))
         out_pool = ctx.enter_context(tc.tile_pool(name="out_pool", bufs=RANKS))
+        rows_pool = ctx.enter_context(tc.tile_pool(name="rows_pool", bufs=5))
         work = ctx.enter_context(tc.tile_pool(name="work", bufs=2))
         totals_pool = ctx.enter_context(tc.tile_pool(name="totals_pool", bufs=4))
         psum_sums = ctx.enter_context(tc.psum_pool(name="psum_sums", bufs=2))
@@ -88,43 +90,51 @@ def tile_ferminetoneelectronlayer_pa_kernel(
         x1 = keep.tile([P, RANKS, D1], BF16)
         pair_tiles = []
 
-        def load_scales(first, scales):
-            passes = scales.shape[0]
-            for quadrant in range(4):
-                nc.sync.dma_start(
-                    out=w_scales[32 * quadrant : 32 * quadrant + 4, first : first + passes, :].bitcast(I32),
-                    in_=scales[:, 4 * quadrant : 4 * quadrant + 4, :].rearrange("g r n -> r g n").bitcast(I32),
-                )
+        scale_loads = [
+            (
+                w_scales[32 * quadrant : 32 * quadrant + 4, first : first + scales.shape[0], :].bitcast(I32),
+                scales[:, 4 * quadrant : 4 * quadrant + 4, :].rearrange("g r n -> r g n").bitcast(I32),
+            )
+            for first, scales in (
+                (PASS_UNMIXED, w_unmixed_scales),
+                (PASS_MIXED, w_mixed_scales),
+                (PASS_2E, w_2e_scales),
+            )
+            for quadrant in range(4)
+        ]
+
+        def load(to, source):
+            nc.sync.dma_start(out=to, in_=source)
+            if scale_loads:
+                scales_to, scales_source = scale_loads[0]
+                scale_loads.remove(scale_loads[0])
+                nc.sync.dma_start(out=scales_to, in_=scales_source)
 
         def load_words(first, words):
-            passes = words.shape[0]
-            nc.sync.dma_start(
-                out=w_words[:, first : first + passes, :].bitcast(I32),
-                in_=words.rearrange("g p n -> p g n").bitcast(I32),
+            load(
+                w_words[:, first : first + words.shape[0], :].bitcast(I32),
+                words.rearrange("g p n -> p g n").bitcast(I32),
             )
 
-        def load_pairs(r, queue):
-            pairs = pair_pool.tile([P, SPINS, GROUPS, ROWS, SPINS, D2], BF16)
+        def load_pairs(r):
+            pairs = pair_pool.tile([P, SPINS, GROUPS, SPINS * ROWS, D2], BF16)
             for s in range(SPINS):
                 for grp in range(GROUPS):
                     for o in range(SPINS):
-                        queue.dma_start(
-                            out=pairs[:, s, grp, :, o, :],
-                            in_=pair_rows[GROUP_WALKERS * grp : GROUP_WALKERS * (grp + 1), s, r, (s + o) % SPINS],
+                        load(
+                            pairs[:, s, grp, ROWS * o : ROWS * (o + 1), :],
+                            pair_rows[GROUP_WALKERS * grp : GROUP_WALKERS * (grp + 1), s, r, (s + o) % SPINS],
                         )
             pair_tiles.append(pairs)
 
         for r in range(0, RANKS, 2):
             nc.sync.dma_start(out=x1[:, r : r + 2, :], in_=x1_rows[:, r : r + 2, :])
         load_words(PASS_UNMIXED, w_unmixed_words)
-        load_scales(PASS_UNMIXED, w_unmixed_scales)
-        load_scales(PASS_MIXED, w_mixed_scales)
-        load_scales(PASS_2E, w_2e_scales)
-        load_pairs(0, nc.sync)
-        load_words(PASS_MIXED, w_mixed_words)
+        for g in range(0, 4, 2):
+            load_words(PASS_MIXED + g, w_mixed_words[g : g + 2])
         load_words(PASS_2E, w_2e_words)
-        for r in range(1, RANKS):
-            load_pairs(r, nc.sync)
+        for r in range(RANKS):
+            load_pairs(r)
 
         def mx_pass(acc, codes, scales, w_pass, half, start, stop):
             nc.tensor.matmul_mx(
@@ -140,12 +150,9 @@ def tile_ferminetoneelectronlayer_pa_kernel(
         x1_grouped = keep.tile([P, RANKS, 2 * K_PASS], BF16, align_bytes=64)
         x1_codes = keep.tile([P, RANKS, 2 * P], U32, align_bytes=64)
         x1_scales = keep.tile([P, RANKS, 2 * P], U8, align_bytes=64)
-        for r in range(RANKS):
+
+        def turn_x1(r, flipped):
             x1_words = x1[:, r, :].bitcast(F32)
-            if r % 2 == 0:
-                flipped = psum_flip.tile([P, 2, 2, P], F32, tag="flip")
-            else:
-                flipped = psum_acc.tile([P, 2, 2, P], F32, tag="acc")
             for g in range(2):
                 for u in range(2):
                     nc.tensor.transpose(
@@ -171,29 +178,52 @@ def tile_ferminetoneelectronlayer_pa_kernel(
         spins_scales = keep.tile([P, SPINS, 2 * P], U8, align_bytes=64)
         mixed = keep.tile([P, D1], F32)
 
-        def sum_spins():
-            own = spins_grouped[:, 0].rearrange("p g q t -> p (g q t)")
-            nc.vector.tensor_tensor(out=running[:], in0=x1_grouped[:, 0, :], in1=x1_grouped[:, 1, :], op=ADD)
-            for r in range(2, RANKS, 2):
-                two_rows = work.tile([P, D1], F32)
-                nc.vector.tensor_tensor(out=two_rows[:], in0=x1_grouped[:, r, :], in1=x1_grouped[:, r + 1, :], op=ADD)
-                total = running[:] if r + 2 < RANKS else own
-                nc.vector.tensor_tensor(out=total, in0=running[:], in1=two_rows[:], op=ADD)
-                if r == 2:
-                    quantise_x1(0, 2)
+        def add_rows(r, flipped):
+            two_rows = rows_pool.tile([P, 2, P, 2, 2], F32, tag="rows")
+            for g in range(2):
+                nc.vector.tensor_tensor(
+                    out=two_rows[:, g],
+                    in0=flipped[:, g].bitcast(BF16).rearrange("p u (q e) -> p q u e", e=2),
+                    in1=x1_grouped[:, r, K_PASS * g : K_PASS * (g + 1)].rearrange("p (q u e) -> p q u e", u=2, e=2),
+                    op=ADD,
+                )
+            return two_rows[:].rearrange("p g q u e -> p (g q u e)")
+
+        pair_rows_of = []
+        for r in range(0, RANKS, 2):
+            even = psum_flip.tile([P, 2, 2, P], F32, tag="flip")
+            turn_x1(r, even)
+            odd = psum_acc.tile([P, 2, 2, P], F32, tag="acc")
+            turn_x1(r + 1, odd)
+            if r % 4 == 0:
+                two_rows = rows_pool.tile([P, D1], F32, tag="rows")
+                nc.gpsimd.tensor_tensor(out=two_rows[:], in0=x1_grouped[:, r, :], in1=x1_grouped[:, r + 1, :], op=ADD)
+                pair_rows_of.append(two_rows[:])
+            else:
+                pair_rows_of.append(add_rows(r, odd))
+            if r == 2:
+                quantise_x1(0, 2)
+        own = spins_grouped[:, 0].rearrange("p g q t -> p (g q t)")
+        nc.vector.tensor_tensor(out=running[:], in0=pair_rows_of[0], in1=pair_rows_of[1], op=ADD)
+        last_rows = rows_pool.tile([P, D1], F32, tag="rows")
+        nc.vector.tensor_tensor(out=last_rows[:], in0=pair_rows_of[2], in1=pair_rows_of[3], op=ADD)
+        nc.vector.tensor_tensor(out=own, in0=running[:], in1=last_rows[:], op=ADD)
+
+        def quantise_spin(o):
+            nc.vector.quantize_mx(
+                out=spins_codes[:, o, :].bitcast(FP8X4),
+                scales=spins_scales[:, o, :],
+                in_=spins_grouped[:, o].rearrange("p g q t -> p (g q t)"),
+            )
 
         def quantise_spins():
-            for s in range(SPINS):
-                nc.scalar.copy(
+            quantise_spin(0)
+            for s, copy in enumerate((nc.vector.tensor_copy, nc.scalar.copy)):
+                copy(
                     out=spins_grouped[:, 1].rearrange("p g (b s) t -> p g b s t", s=SPINS)[:, :, :, s, :],
                     in_=spins_grouped[:, 0].rearrange("p g (b s) t -> p g b s t", s=SPINS)[:, :, :, 1 - s, :],
                 )
-            for o in range(SPINS):
-                nc.vector.quantize_mx(
-                    out=spins_codes[:, o, :].bitcast(FP8X4),
-                    scales=spins_scales[:, o, :],
-                    in_=spins_grouped[:, o].rearrange("p g q t -> p (g q t)"),
-                )
+            quantise_spin(1)
 
         def spread_bias():
             for half in range(HALVES):
@@ -203,13 +233,12 @@ def tile_ferminetoneelectronlayer_pa_kernel(
                 nc.scalar.copy(out=mixed[:, cols], in_=bias_acc[:])
 
         def mixed_term():
-            for half in range(HALVES):
-                cols = slice(N_HALF * half, N_HALF * (half + 1))
-                acc = psum_flip.tile([P, N_HALF], F32, tag="flip")
-                for o in range(SPINS):
+            accs = [psum_flip.tile([P, N_HALF], F32, name="mixed_acc", tag="flip") for half in range(HALVES)]
+            for o in range(SPINS):
+                for half in range(HALVES):
                     for g in range(2):
                         mx_pass(
-                            acc[:],
+                            accs[half][:],
                             spins_codes[:, o, P * g : P * (g + 1)],
                             spins_scales[:, o, P * g : P * (g + 1)],
                             PASS_MIXED + 2 * o + g,
@@ -217,9 +246,11 @@ def tile_ferminetoneelectronlayer_pa_kernel(
                             o + g == 0,
                             o + g == 2,
                         )
+            for half in range(HALVES):
+                cols = slice(N_HALF * half, N_HALF * (half + 1))
                 nc.vector.scalar_tensor_tensor(
                     out=mixed[:, cols],
-                    in0=acc[:],
+                    in0=accs[half][:],
                     scalar=1.0 / RANKS,
                     in1=mixed[:, cols],
                     op0=mybir.AluOpType.mult,
@@ -230,20 +261,30 @@ def tile_ferminetoneelectronlayer_pa_kernel(
         pair_scales = keep.tile([P, RANKS, P], U8, align_bytes=64)
         pair_sums_of = {}
 
+        outer_of = {}
+
+        def join_outer(r, copy):
+            outer = outer_pool.tile([P, SPINS, GROUPS, SPINS, D2], BF16)
+            copy(
+                out=outer[:].rearrange("p s g o d -> p (s g) o d"),
+                in_=pair_tiles[r][:].rearrange("p s g x d -> p (s g) x d")[:, :, 0 : SPINS * ROWS : SPINS * ROWS - 1, :],
+            )
+            outer_of[r] = outer
+
         def average_pairs(r):
-            pairs = pair_tiles[r]
             pair_sums = psum_sums.tile([P, PACK, SPINS, WALKERS], F32)
             for s in range(SPINS):
                 for grp in range(GROUPS):
+                    inner = pair_tiles[r][:, s, grp, 1:3, :].rearrange("p o d -> p (o d)")
+                    outer = outer_of[r][:, s, grp].rearrange("p o d -> p (o d)")
                     for t in range(PACK):
-                        for a in range(ROWS):
-                            row = pairs[:, s, grp, a].rearrange("p o d -> p (o d)")
+                        for row in (inner, outer):
                             nc.tensor.matmul(
                                 out=pair_sums[:, t, s, GROUP_WALKERS * grp : GROUP_WALKERS * (grp + 1)],
                                 lhsT=row[:, t : SPINS * D2 : PACK],
                                 rhs=averager[:],
-                                start=(a == 0),
-                                stop=(a == ROWS - 1),
+                                start=row is inner,
+                                stop=row is outer,
                             )
             pair_sums_of[r] = pair_sums
 
@@ -299,26 +340,29 @@ def tile_ferminetoneelectronlayer_pa_kernel(
 
         def add_skip(r):
             result = out_pool.tile([P, D1], F32)
-            adder = nc.vector if r == RANKS - 1 else nc.gpsimd
             for half in range(HALVES):
                 cols = slice(N_HALF * half, N_HALF * (half + 1))
+                adder = nc.vector if r == RANKS - 1 or (r % 2 == 1 and half == 1) else nc.gpsimd
                 adder.tensor_tensor(out=result[:, cols], in0=totals_of[r][half][:], in1=x1[:, r, cols], op=ADD)
                 nc.sync.dma_start(out=out_rows[:, r, cols], in_=result[:, cols])
 
-        sum_spins()
         spread_bias()
         start_tile(0)
         start_tile(1)
+        join_outer(0, nc.scalar.copy)
         average_pairs(0)
         quantise_spins()
         quantise_x1(2, 2)
         group_pairs(0)
         quantise_pairs(0)
         quantise_x1(4, 4)
+        join_outer(1, nc.scalar.copy)
         mixed_term()
-        average_pairs(1)
+        join_outer(2, nc.vector.tensor_copy)
         for r in range(RANKS):
             add_pairs(r)
+            if r == 0:
+                average_pairs(1)
             if r + 2 < RANKS:
                 average_pairs(r + 2)
             if r + 1 < RANKS:
@@ -329,3 +373,5 @@ def tile_ferminetoneelectronlayer_pa_kernel(
             add_skip(r)
             if r + 2 < RANKS:
                 start_tile(r + 2)
+            if r + 3 < RANKS:
+                join_outer(r + 3, nc.vector.tensor_copy)

@@ -25,6 +25,7 @@ K_PASS = 512
 GROUPS = 2
 GROUP_WALKERS = WALKERS // GROUPS
 ROWS = 2
+READY_TILES = 2
 PACK = 4
 
 PASS_UNMIXED = 0
@@ -54,10 +55,10 @@ def tile_ferminetoneelectronlayer_pa_kernel(
         keep = ctx.enter_context(tc.tile_pool(name="keep", bufs=1))
         pair_pool = ctx.enter_context(tc.tile_pool(name="pair_pool", bufs=RANKS))
         outer_pool = ctx.enter_context(tc.tile_pool(name="outer_pool", bufs=3))
-        out_pool = ctx.enter_context(tc.tile_pool(name="out_pool", bufs=RANKS))
+        out_pool = ctx.enter_context(tc.tile_pool(name="out_pool", bufs=2 * RANKS))
         rows_pool = ctx.enter_context(tc.tile_pool(name="rows_pool", bufs=5))
         work = ctx.enter_context(tc.tile_pool(name="work", bufs=2))
-        totals_pool = ctx.enter_context(tc.tile_pool(name="totals_pool", bufs=4))
+        totals_pool = ctx.enter_context(tc.tile_pool(name="totals_pool", bufs=6))
         psum_sums = ctx.enter_context(tc.psum_pool(name="psum_sums", bufs=2))
         psum_flip = ctx.enter_context(tc.psum_pool(name="psum_flip", bufs=2))
         psum_acc = ctx.enter_context(tc.psum_pool(name="psum_acc", bufs=4))
@@ -97,8 +98,8 @@ def tile_ferminetoneelectronlayer_pa_kernel(
             )
             for first, scales in (
                 (PASS_UNMIXED, w_unmixed_scales),
-                (PASS_MIXED, w_mixed_scales),
                 (PASS_2E, w_2e_scales),
+                (PASS_MIXED, w_mixed_scales),
             )
             for quadrant in range(4)
         ]
@@ -121,8 +122,9 @@ def tile_ferminetoneelectronlayer_pa_kernel(
             for s in range(SPINS):
                 for grp in range(GROUPS):
                     for o in range(SPINS):
+                        rows = slice(o, SPINS * ROWS, SPINS) if r < READY_TILES else slice(ROWS * o, ROWS * (o + 1))
                         load(
-                            pairs[:, s, grp, ROWS * o : ROWS * (o + 1), :],
+                            pairs[:, s, grp, rows, :],
                             pair_rows[GROUP_WALKERS * grp : GROUP_WALKERS * (grp + 1), s, r, (s + o) % SPINS],
                         )
             pair_tiles.append(pairs)
@@ -130,10 +132,11 @@ def tile_ferminetoneelectronlayer_pa_kernel(
         for r in range(0, RANKS, 2):
             nc.sync.dma_start(out=x1[:, r : r + 2, :], in_=x1_rows[:, r : r + 2, :])
         load_words(PASS_UNMIXED, w_unmixed_words)
+        load_words(PASS_2E, w_2e_words)
+        load_pairs(0)
         for g in range(0, 4, 2):
             load_words(PASS_MIXED + g, w_mixed_words[g : g + 2])
-        load_words(PASS_2E, w_2e_words)
-        for r in range(RANKS):
+        for r in range(1, RANKS):
             load_pairs(r)
 
         def mx_pass(acc, codes, scales, w_pass, half, start, stop):
@@ -263,9 +266,9 @@ def tile_ferminetoneelectronlayer_pa_kernel(
 
         outer_of = {}
 
-        def join_outer(r, copy):
+        def join_outer(r):
             outer = outer_pool.tile([P, SPINS, GROUPS, SPINS, D2], BF16)
-            copy(
+            nc.vector.tensor_copy(
                 out=outer[:].rearrange("p s g o d -> p (s g) o d"),
                 in_=pair_tiles[r][:].rearrange("p s g x d -> p (s g) x d")[:, :, 0 : SPINS * ROWS : SPINS * ROWS - 1, :],
             )
@@ -275,16 +278,19 @@ def tile_ferminetoneelectronlayer_pa_kernel(
             pair_sums = psum_sums.tile([P, PACK, SPINS, WALKERS], F32)
             for s in range(SPINS):
                 for grp in range(GROUPS):
-                    inner = pair_tiles[r][:, s, grp, 1:3, :].rearrange("p o d -> p (o d)")
-                    outer = outer_of[r][:, s, grp].rearrange("p o d -> p (o d)")
+                    pairs = pair_tiles[r][:, s, grp]
+                    if r < READY_TILES:
+                        joined = (pairs[:, 0:2, :], pairs[:, 2:4, :])
+                    else:
+                        joined = (pairs[:, 1:3, :], outer_of[r][:, s, grp])
                     for t in range(PACK):
-                        for row in (inner, outer):
+                        for a in range(ROWS):
                             nc.tensor.matmul(
                                 out=pair_sums[:, t, s, GROUP_WALKERS * grp : GROUP_WALKERS * (grp + 1)],
-                                lhsT=row[:, t : SPINS * D2 : PACK],
+                                lhsT=joined[a].rearrange("p o d -> p (o d)")[:, t : SPINS * D2 : PACK],
                                 rhs=averager[:],
-                                start=row is inner,
-                                stop=row is outer,
+                                start=(a == 0),
+                                stop=(a == ROWS - 1),
                             )
             pair_sums_of[r] = pair_sums
 
@@ -338,40 +344,46 @@ def tile_ferminetoneelectronlayer_pa_kernel(
                 totals.append(total)
             totals_of[r] = totals
 
-        def add_skip(r):
-            result = out_pool.tile([P, D1], F32)
-            for half in range(HALVES):
-                cols = slice(N_HALF * half, N_HALF * (half + 1))
-                adder = nc.vector if r == RANKS - 1 or (r % 2 == 1 and half == 1) else nc.gpsimd
-                adder.tensor_tensor(out=result[:, cols], in0=totals_of[r][half][:], in1=x1[:, r, cols], op=ADD)
-                nc.sync.dma_start(out=out_rows[:, r, cols], in_=result[:, cols])
+        def add_skip(r, half, adder):
+            result = out_pool.tile([P, N_HALF], F32)
+            cols = slice(N_HALF * half, N_HALF * (half + 1))
+            adder.tensor_tensor(out=result[:], in0=totals_of[r][half][:], in1=x1[:, r, cols], op=ADD)
+            nc.sync.dma_start(out=out_rows[:, r, cols], in_=result[:])
 
-        spread_bias()
+        def skip_on_vector(r):
+            return r % 2 == 1 or r == RANKS - 2
+
         start_tile(0)
         start_tile(1)
-        join_outer(0, nc.scalar.copy)
         average_pairs(0)
-        quantise_spins()
-        quantise_x1(2, 2)
+        spread_bias()
         group_pairs(0)
+        quantise_spins()
         quantise_pairs(0)
-        quantise_x1(4, 4)
-        join_outer(1, nc.scalar.copy)
+        quantise_x1(2, 2)
         mixed_term()
-        join_outer(2, nc.vector.tensor_copy)
+        quantise_x1(4, 4)
+        join_outer(2)
         for r in range(RANKS):
             add_pairs(r)
             if r == 0:
                 average_pairs(1)
+                group_pairs(1)
             if r + 2 < RANKS:
                 average_pairs(r + 2)
-            if r + 1 < RANKS:
-                group_pairs(r + 1)
             add_mixed(r)
-            if r + 1 < RANKS:
-                quantise_pairs(r + 1)
-            add_skip(r)
+            if r == 0:
+                quantise_pairs(1)
+            add_skip(r, 0, nc.gpsimd)
+            if r > 0 and skip_on_vector(r - 1):
+                add_skip(r - 1, 1, nc.vector)
+            if not skip_on_vector(r):
+                add_skip(r, 1, nc.gpsimd)
             if r + 2 < RANKS:
                 start_tile(r + 2)
             if r + 3 < RANKS:
-                join_outer(r + 3, nc.vector.tensor_copy)
+                join_outer(r + 3)
+            if r + 2 < RANKS:
+                group_pairs(r + 2)
+                quantise_pairs(r + 2)
+        add_skip(RANKS - 1, 1, nc.vector)

@@ -25,7 +25,6 @@ K_PASS = 512
 GROUPS = 2
 GROUP_WALKERS = WALKERS // GROUPS
 ROWS = 2
-READY_TILES = 2
 PACK = 4
 
 PASS_UNMIXED = 0
@@ -54,7 +53,6 @@ def tile_ferminetoneelectronlayer_pa_kernel(
         const = ctx.enter_context(tc.tile_pool(name="const", bufs=1))
         keep = ctx.enter_context(tc.tile_pool(name="keep", bufs=1))
         pair_pool = ctx.enter_context(tc.tile_pool(name="pair_pool", bufs=RANKS))
-        outer_pool = ctx.enter_context(tc.tile_pool(name="outer_pool", bufs=3))
         out_pool = ctx.enter_context(tc.tile_pool(name="out_pool", bufs=2 * RANKS))
         rows_pool = ctx.enter_context(tc.tile_pool(name="rows_pool", bufs=5))
         work = ctx.enter_context(tc.tile_pool(name="work", bufs=2))
@@ -118,13 +116,12 @@ def tile_ferminetoneelectronlayer_pa_kernel(
             )
 
         def load_pairs(r):
-            pairs = pair_pool.tile([P, SPINS, GROUPS, SPINS * ROWS, D2], BF16)
+            pairs = pair_pool.tile([P, SPINS, GROUPS, ROWS, SPINS, D2], BF16)
             for s in range(SPINS):
                 for grp in range(GROUPS):
                     for o in range(SPINS):
-                        rows = slice(o, SPINS * ROWS, SPINS) if r < READY_TILES else slice(ROWS * o, ROWS * (o + 1))
                         load(
-                            pairs[:, s, grp, rows, :],
+                            pairs[:, s, grp, :, o, :],
                             pair_rows[GROUP_WALKERS * grp : GROUP_WALKERS * (grp + 1), s, r, (s + o) % SPINS],
                         )
             pair_tiles.append(pairs)
@@ -264,30 +261,17 @@ def tile_ferminetoneelectronlayer_pa_kernel(
         pair_scales = keep.tile([P, RANKS, P], U8, align_bytes=64)
         pair_sums_of = {}
 
-        outer_of = {}
-
-        def join_outer(r):
-            outer = outer_pool.tile([P, SPINS, GROUPS, SPINS, D2], BF16)
-            nc.vector.tensor_copy(
-                out=outer[:].rearrange("p s g o d -> p (s g) o d"),
-                in_=pair_tiles[r][:].rearrange("p s g x d -> p (s g) x d")[:, :, 0 : SPINS * ROWS : SPINS * ROWS - 1, :],
-            )
-            outer_of[r] = outer
-
         def average_pairs(r):
+            pairs = pair_tiles[r]
             pair_sums = psum_sums.tile([P, PACK, SPINS, WALKERS], F32)
             for s in range(SPINS):
                 for grp in range(GROUPS):
-                    pairs = pair_tiles[r][:, s, grp]
-                    if r < READY_TILES:
-                        joined = (pairs[:, 0:2, :], pairs[:, 2:4, :])
-                    else:
-                        joined = (pairs[:, 1:3, :], outer_of[r][:, s, grp])
                     for t in range(PACK):
                         for a in range(ROWS):
+                            row = pairs[:, s, grp, a].rearrange("p o d -> p (o d)")
                             nc.tensor.matmul(
                                 out=pair_sums[:, t, s, GROUP_WALKERS * grp : GROUP_WALKERS * (grp + 1)],
-                                lhsT=joined[a].rearrange("p o d -> p (o d)")[:, t : SPINS * D2 : PACK],
+                                lhsT=row[:, t : SPINS * D2 : PACK],
                                 rhs=averager[:],
                                 start=(a == 0),
                                 stop=(a == ROWS - 1),
@@ -344,14 +328,12 @@ def tile_ferminetoneelectronlayer_pa_kernel(
                 totals.append(total)
             totals_of[r] = totals
 
-        def add_skip(r, half, adder):
-            result = out_pool.tile([P, N_HALF], F32)
-            cols = slice(N_HALF * half, N_HALF * (half + 1))
-            adder.tensor_tensor(out=result[:], in0=totals_of[r][half][:], in1=x1[:, r, cols], op=ADD)
-            nc.sync.dma_start(out=out_rows[:, r, cols], in_=result[:])
-
-        def skip_on_vector(r):
-            return r % 2 == 1 or r == RANKS - 2
+        def add_skip(r):
+            for half in range(HALVES):
+                result = out_pool.tile([P, N_HALF], F32)
+                cols = slice(N_HALF * half, N_HALF * (half + 1))
+                nc.vector.tensor_tensor(out=result[:], in0=totals_of[r][half][:], in1=x1[:, r, cols], op=ADD)
+                nc.sync.dma_start(out=out_rows[:, r, cols], in_=result[:])
 
         start_tile(0)
         start_tile(1)
@@ -363,7 +345,6 @@ def tile_ferminetoneelectronlayer_pa_kernel(
         quantise_x1(2, 2)
         mixed_term()
         quantise_x1(4, 4)
-        join_outer(2)
         for r in range(RANKS):
             add_pairs(r)
             if r == 0:
@@ -374,16 +355,11 @@ def tile_ferminetoneelectronlayer_pa_kernel(
             add_mixed(r)
             if r == 0:
                 quantise_pairs(1)
-            add_skip(r, 0, nc.gpsimd)
-            if r > 0 and skip_on_vector(r - 1):
-                add_skip(r - 1, 1, nc.vector)
-            if not skip_on_vector(r):
-                add_skip(r, 1, nc.gpsimd)
+            if r > 0:
+                add_skip(r - 1)
             if r + 2 < RANKS:
                 start_tile(r + 2)
-            if r + 3 < RANKS:
-                join_outer(r + 3)
             if r + 2 < RANKS:
                 group_pairs(r + 2)
                 quantise_pairs(r + 2)
-        add_skip(RANKS - 1, 1, nc.vector)
+        add_skip(RANKS - 1)

@@ -25,6 +25,7 @@ K_PASS = 512
 GROUPS = 2
 GROUP_WALKERS = WALKERS // GROUPS
 ROWS = 2
+JOINED_TILES = 2
 PACK = 4
 
 PASS_UNMIXED = 0
@@ -53,7 +54,8 @@ def tile_ferminetoneelectronlayer_pa_kernel(
         const = ctx.enter_context(tc.tile_pool(name="const", bufs=1))
         keep = ctx.enter_context(tc.tile_pool(name="keep", bufs=1))
         pair_pool = ctx.enter_context(tc.tile_pool(name="pair_pool", bufs=RANKS))
-        out_pool = ctx.enter_context(tc.tile_pool(name="out_pool", bufs=2 * RANKS))
+        outer_pool = ctx.enter_context(tc.tile_pool(name="outer_pool", bufs=4))
+        out_pool = ctx.enter_context(tc.tile_pool(name="out_pool", bufs=RANKS))
         rows_pool = ctx.enter_context(tc.tile_pool(name="rows_pool", bufs=5))
         work = ctx.enter_context(tc.tile_pool(name="work", bufs=2))
         totals_pool = ctx.enter_context(tc.tile_pool(name="totals_pool", bufs=6))
@@ -72,7 +74,6 @@ def tile_ferminetoneelectronlayer_pa_kernel(
         make_identity(nc, ident_f32[:])
         bias_row = keep.tile([P, D1], BF16)
         nc.gpsimd.memset(bias_row[:], 0.0)
-        nc.gpsimd.dma_start(out=bias_row[0:1, :], in_=b_unmixed.unsqueeze(0))
         ones = const.tile([P, P], BF16)
         nc.gpsimd.memset(ones[:], 1.0)
         member = const.tile([P, GROUP_WALKERS], F32)
@@ -116,18 +117,20 @@ def tile_ferminetoneelectronlayer_pa_kernel(
             )
 
         def load_pairs(r):
-            pairs = pair_pool.tile([P, SPINS, GROUPS, ROWS, SPINS, D2], BF16)
+            pairs = pair_pool.tile([P, SPINS, GROUPS, SPINS * ROWS, D2], BF16)
             for s in range(SPINS):
                 for grp in range(GROUPS):
                     for o in range(SPINS):
+                        rows = slice(ROWS * o, ROWS * (o + 1)) if r < JOINED_TILES else slice(o, SPINS * ROWS, SPINS)
                         load(
-                            pairs[:, s, grp, :, o, :],
+                            pairs[:, s, grp, rows, :],
                             pair_rows[GROUP_WALKERS * grp : GROUP_WALKERS * (grp + 1), s, r, (s + o) % SPINS],
                         )
             pair_tiles.append(pairs)
 
         for r in range(0, RANKS, 2):
             nc.sync.dma_start(out=x1[:, r : r + 2, :], in_=x1_rows[:, r : r + 2, :])
+        nc.sync.dma_start(out=bias_row[0:1, :], in_=b_unmixed.unsqueeze(0))
         load_words(PASS_UNMIXED, w_unmixed_words)
         load_words(PASS_2E, w_2e_words)
         load_pairs(0)
@@ -151,7 +154,7 @@ def tile_ferminetoneelectronlayer_pa_kernel(
         x1_codes = keep.tile([P, RANKS, 2 * P], U32, align_bytes=64)
         x1_scales = keep.tile([P, RANKS, 2 * P], U8, align_bytes=64)
 
-        def turn_x1(r, flipped):
+        def turn_x1(r, flipped, copy):
             x1_words = x1[:, r, :].bitcast(F32)
             for g in range(2):
                 for u in range(2):
@@ -160,7 +163,7 @@ def tile_ferminetoneelectronlayer_pa_kernel(
                         x1_words[:, 256 * g + u : 256 * (g + 1) : 2],
                         ident_f32[:],
                     )
-            nc.scalar.copy(
+            copy(
                 out=x1_grouped[:, r, :].bitcast(F32).rearrange("p (g q u) -> p g q u", g=2, u=2),
                 in_=flipped[:].rearrange("p g u q -> p g q u"),
             )
@@ -192,9 +195,10 @@ def tile_ferminetoneelectronlayer_pa_kernel(
         pair_rows_of = []
         for r in range(0, RANKS, 2):
             even = psum_flip.tile([P, 2, 2, P], F32, tag="flip")
-            turn_x1(r, even)
+            copy = nc.vector.tensor_copy if r == 0 else nc.scalar.copy
+            turn_x1(r, even, copy)
             odd = psum_acc.tile([P, 2, 2, P], F32, tag="acc")
-            turn_x1(r + 1, odd)
+            turn_x1(r + 1, odd, copy)
             if r % 4 == 0:
                 two_rows = rows_pool.tile([P, D1], F32, tag="rows")
                 nc.gpsimd.tensor_tensor(out=two_rows[:], in0=x1_grouped[:, r, :], in1=x1_grouped[:, r + 1, :], op=ADD)
@@ -261,17 +265,31 @@ def tile_ferminetoneelectronlayer_pa_kernel(
         pair_scales = keep.tile([P, RANKS, P], U8, align_bytes=64)
         pair_sums_of = {}
 
+        outer_of = {}
+
+        def join_outer(r):
+            outer = outer_pool.tile([P, SPINS, GROUPS, SPINS, D2], BF16)
+            for o in range(SPINS):
+                nc.scalar.copy(
+                    out=outer[:, :, :, o, :].rearrange("p s g d -> p (s g) d"),
+                    in_=pair_tiles[r][:, :, :, 3 * o, :].rearrange("p s g d -> p (s g) d"),
+                )
+            outer_of[r] = outer
+
         def average_pairs(r):
-            pairs = pair_tiles[r]
             pair_sums = psum_sums.tile([P, PACK, SPINS, WALKERS], F32)
             for s in range(SPINS):
                 for grp in range(GROUPS):
+                    pairs = pair_tiles[r][:, s, grp]
+                    if r < JOINED_TILES:
+                        joined = (pairs[:, 1:3, :], outer_of[r][:, s, grp])
+                    else:
+                        joined = (pairs[:, 0:2, :], pairs[:, 2:4, :])
                     for t in range(PACK):
                         for a in range(ROWS):
-                            row = pairs[:, s, grp, a].rearrange("p o d -> p (o d)")
                             nc.tensor.matmul(
                                 out=pair_sums[:, t, s, GROUP_WALKERS * grp : GROUP_WALKERS * (grp + 1)],
-                                lhsT=row[:, t : SPINS * D2 : PACK],
+                                lhsT=joined[a].rearrange("p o d -> p (o d)")[:, t : SPINS * D2 : PACK],
                                 rhs=averager[:],
                                 start=(a == 0),
                                 stop=(a == ROWS - 1),
@@ -295,58 +313,70 @@ def tile_ferminetoneelectronlayer_pa_kernel(
         acc_of = {}
         totals_of = {}
 
-        def start_tile(r):
-            accs = []
-            for half in range(HALVES):
-                acc = psum_acc.tile([P, N_HALF], F32, tag="acc")
-                for g in range(2):
-                    mx_pass(
-                        acc[:],
-                        x1_codes[:, r, P * g : P * (g + 1)],
-                        x1_scales[:, r, P * g : P * (g + 1)],
-                        PASS_UNMIXED + g,
-                        half,
-                        g == 0,
-                        False,
-                    )
-                accs.append(acc)
-            acc_of[r] = accs
+        def start_half(r, half):
+            acc = psum_acc.tile([P, N_HALF], F32, tag="acc")
+            for g in range(2):
+                mx_pass(
+                    acc[:],
+                    x1_codes[:, r, P * g : P * (g + 1)],
+                    x1_scales[:, r, P * g : P * (g + 1)],
+                    PASS_UNMIXED + g,
+                    half,
+                    g == 0,
+                    False,
+                )
+            acc_of[r, half] = acc
 
-        def add_pairs(r):
+        def start_tile(r):
             for half in range(HALVES):
-                acc = acc_of[r][half]
-                mx_pass(acc[:], pair_codes[:, r, :], pair_scales[:, r, :], PASS_2E, half, False, True)
+                start_half(r, half)
+
+        def add_pairs(r, half):
+            acc = acc_of[r, half]
+            mx_pass(acc[:], pair_codes[:, r, :], pair_scales[:, r, :], PASS_2E, half, False, True)
 
         def add_mixed(r):
             totals = []
             for half in range(HALVES):
                 total = totals_pool.tile([P, N_HALF], F32)
                 nc.vector.tensor_tensor(
-                    out=total[:], in0=acc_of[r][half][:], in1=mixed[:, N_HALF * half : N_HALF * (half + 1)], op=ADD
+                    out=total[:], in0=acc_of[r, half][:], in1=mixed[:, N_HALF * half : N_HALF * (half + 1)], op=ADD
                 )
                 nc.scalar.activation(out=total[:], in_=total[:], func=ACT.Tanh)
                 totals.append(total)
             totals_of[r] = totals
 
         def add_skip(r):
+            adder = nc.gpsimd if RANKS - 3 <= r < RANKS - 1 else nc.vector
+            result = out_pool.tile([P, D1], F32)
+            by_half = r >= RANKS - 3
             for half in range(HALVES):
-                result = out_pool.tile([P, N_HALF], F32)
                 cols = slice(N_HALF * half, N_HALF * (half + 1))
-                nc.vector.tensor_tensor(out=result[:], in0=totals_of[r][half][:], in1=x1[:, r, cols], op=ADD)
-                nc.sync.dma_start(out=out_rows[:, r, cols], in_=result[:])
+                adder.tensor_tensor(out=result[:, cols], in0=totals_of[r][half][:], in1=x1[:, r, cols], op=ADD)
+                if by_half:
+                    nc.sync.dma_start(out=out_rows[:, r, cols], in_=result[:, cols])
+            if not by_half:
+                nc.sync.dma_start(out=out_rows[:, r, :], in_=result[:])
 
+        spread_bias()
         start_tile(0)
         start_tile(1)
+        join_outer(0)
         average_pairs(0)
-        spread_bias()
-        group_pairs(0)
         quantise_spins()
-        quantise_pairs(0)
+        group_pairs(0)
         quantise_x1(2, 2)
+        quantise_pairs(0)
         mixed_term()
         quantise_x1(4, 4)
+        join_outer(1)
         for r in range(RANKS):
-            add_pairs(r)
+            for half in range(HALVES):
+                if r == RANKS - 1:
+                    start_half(r, half)
+                add_pairs(r, half)
+            if 0 < r < RANKS - 2:
+                start_tile(r + 1)
             if r == 0:
                 average_pairs(1)
                 group_pairs(1)
@@ -357,8 +387,6 @@ def tile_ferminetoneelectronlayer_pa_kernel(
                 quantise_pairs(1)
             if r > 0:
                 add_skip(r - 1)
-            if r + 2 < RANKS:
-                start_tile(r + 2)
             if r + 2 < RANKS:
                 group_pairs(r + 2)
                 quantise_pairs(r + 2)

@@ -105,10 +105,10 @@ def tile_ferminetoneelectronlayer_pa_kernel(
 
         def load(to, source):
             nc.sync.dma_start(out=to, in_=source)
-            if scale_loads:
-                scales_to, scales_source = scale_loads[0]
-                scale_loads.remove(scale_loads[0])
-                nc.sync.dma_start(out=scales_to, in_=scales_source)
+
+        def load_scales(first, last):
+            for to, source in scale_loads[first:last]:
+                load(to, source)
 
         def load_words(first, words):
             load(
@@ -130,12 +130,16 @@ def tile_ferminetoneelectronlayer_pa_kernel(
 
         for r in range(0, RANKS, 2):
             nc.sync.dma_start(out=x1[:, r : r + 2, :], in_=x1_rows[:, r : r + 2, :])
+        load_scales(0, 4)
         nc.sync.dma_start(out=bias_row[0:1, :], in_=b_unmixed.unsqueeze(0))
         load_words(PASS_UNMIXED, w_unmixed_words)
         load_words(PASS_2E, w_2e_words)
+        load_scales(4, 6)
         load_pairs(0)
-        for g in range(0, 4, 2):
-            load_words(PASS_MIXED + g, w_mixed_words[g : g + 2])
+        load_words(PASS_MIXED + 0, w_mixed_words[0 : 2])
+        load_scales(6, 9)
+        load_words(PASS_MIXED + 2, w_mixed_words[2 : 4])
+        load_scales(9, 12)
         for r in range(1, RANKS):
             load_pairs(r)
 
@@ -347,12 +351,11 @@ def tile_ferminetoneelectronlayer_pa_kernel(
             totals_of[r] = totals
 
         def add_skip(r):
-            adder = nc.gpsimd if RANKS - 3 <= r < RANKS - 1 else nc.vector
             result = out_pool.tile([P, D1], F32)
             by_half = r >= RANKS - 3
             for half in range(HALVES):
                 cols = slice(N_HALF * half, N_HALF * (half + 1))
-                adder.tensor_tensor(out=result[:, cols], in0=totals_of[r][half][:], in1=x1[:, r, cols], op=ADD)
+                nc.vector.tensor_tensor(out=result[:, cols], in0=totals_of[r][half][:], in1=x1[:, r, cols], op=ADD)
                 if by_half:
                     nc.sync.dma_start(out=out_rows[:, r, cols], in_=result[:, cols])
             if not by_half:

@@ -68,7 +68,7 @@ def tile_ferminetoneelectronlayer_pa_kernel(
         out_rows = out.flatten_outer_dims().rearrange("(q r) n -> q r n", r=RANKS)
         pair_rows = in_2e.rearrange("b (s r) (c j a) d -> b s r c j a d", s=SPINS, c=SPINS, a=ROWS)
 
-        w_scales = keep.tile([P, PASSES, D1], U8, align_bytes=64)
+        w_scales = keep.tile([P, PASSES, D1], U8, align_bytes=256)
         nc.vector.memset(w_scales[:].bitcast(I32), 0)
         ident_f32 = const.tile([P, P], F32)
         make_identity(nc, ident_f32[:])
@@ -86,7 +86,7 @@ def tile_ferminetoneelectronlayer_pa_kernel(
         averager = const.tile([P, GROUP_WALKERS], BF16)
         nc.vector.tensor_scalar_mul(out=averager[:], in0=member[:], scalar1=1.0 / RANKS)
 
-        w_words = keep.tile([P, PASSES, 2 * D1], U8, align_bytes=64)
+        w_words = keep.tile([P, PASSES, 2 * D1], U8, align_bytes=256)
         x1 = keep.tile([P, RANKS, D1], BF16)
         pair_tiles = []
 
@@ -155,8 +155,8 @@ def tile_ferminetoneelectronlayer_pa_kernel(
             )
 
         x1_grouped = keep.tile([P, RANKS, 2 * K_PASS], BF16, align_bytes=64)
-        x1_codes = keep.tile([P, RANKS, 2 * P], U32, align_bytes=64)
-        x1_scales = keep.tile([P, RANKS, 2 * P], U8, align_bytes=64)
+        x1_codes = keep.tile([P, RANKS, 2 * P], U32, align_bytes=256)
+        x1_scales = keep.tile([P, RANKS, 2 * P], U8, align_bytes=256)
 
         def turn_x1(r, flipped, copy):
             x1_words = x1[:, r, :].bitcast(F32)
@@ -181,8 +181,8 @@ def tile_ferminetoneelectronlayer_pa_kernel(
 
         running = keep.tile([P, D1], F32)
         spins_grouped = keep.tile([P, SPINS, 2, P, PACK], BF16, align_bytes=64)
-        spins_codes = keep.tile([P, SPINS, 2 * P], U32, align_bytes=64)
-        spins_scales = keep.tile([P, SPINS, 2 * P], U8, align_bytes=64)
+        spins_codes = keep.tile([P, SPINS, 2 * P], U32, align_bytes=256)
+        spins_scales = keep.tile([P, SPINS, 2 * P], U8, align_bytes=256)
         mixed = keep.tile([P, D1], F32)
 
         def add_rows(r, flipped):
@@ -265,8 +265,8 @@ def tile_ferminetoneelectronlayer_pa_kernel(
                     op1=ADD,
                 )
 
-        pair_codes = keep.tile([P, RANKS, P], U32, align_bytes=64)
-        pair_scales = keep.tile([P, RANKS, P], U8, align_bytes=64)
+        pair_codes = keep.tile([P, RANKS, P], U32, align_bytes=256)
+        pair_scales = keep.tile([P, RANKS, P], U8, align_bytes=256)
         pair_sums_of = {}
 
         outer_of = {}
@@ -355,7 +355,8 @@ def tile_ferminetoneelectronlayer_pa_kernel(
             by_half = r >= RANKS - 3
             for half in range(HALVES):
                 cols = slice(N_HALF * half, N_HALF * (half + 1))
-                nc.vector.tensor_tensor(out=result[:, cols], in0=totals_of[r][half][:], in1=x1[:, r, cols], op=ADD)
+                adder = nc.gpsimd if half == 0 and RANKS - 3 <= r < RANKS - 1 else nc.vector
+                adder.tensor_tensor(out=result[:, cols], in0=totals_of[r][half][:], in1=x1[:, r, cols], op=ADD)
                 if by_half:
                     nc.sync.dma_start(out=out_rows[:, r, cols], in_=result[:, cols])
             if not by_half:

@@ -25,7 +25,6 @@ K_PASS = 512
 GROUPS = 2
 GROUP_WALKERS = WALKERS // GROUPS
 ROWS = 2
-JOINED_TILES = 2
 PACK = 4
 
 PASS_UNMIXED = 0
@@ -90,6 +89,10 @@ def tile_ferminetoneelectronlayer_pa_kernel(
         x1 = keep.tile([P, RANKS, D1], BF16)
         pair_tiles = []
 
+        def joined_tile(r):
+            return r < 2 or r in (4, 6)
+
+
         scale_loads = [
             (
                 w_scales[32 * quadrant : 32 * quadrant + 4, first : first + scales.shape[0], :].bitcast(I32),
@@ -121,7 +124,7 @@ def tile_ferminetoneelectronlayer_pa_kernel(
             for s in range(SPINS):
                 for grp in range(GROUPS):
                     for o in range(SPINS):
-                        rows = slice(ROWS * o, ROWS * (o + 1)) if r < JOINED_TILES else slice(o, SPINS * ROWS, SPINS)
+                        rows = slice(ROWS * o, ROWS * (o + 1)) if joined_tile(r) else slice(o, SPINS * ROWS, SPINS)
                         load(
                             pairs[:, s, grp, rows, :],
                             pair_rows[GROUP_WALKERS * grp : GROUP_WALKERS * (grp + 1), s, r, (s + o) % SPINS],
@@ -274,10 +277,12 @@ def tile_ferminetoneelectronlayer_pa_kernel(
         def join_outer(r):
             outer = outer_pool.tile([P, SPINS, GROUPS, SPINS, D2], BF16)
             for o in range(SPINS):
-                nc.scalar.copy(
-                    out=outer[:, :, :, o, :].rearrange("p s g d -> p (s g) d"),
-                    in_=pair_tiles[r][:, :, :, 3 * o, :].rearrange("p s g d -> p (s g) d"),
-                )
+                to = outer[:, :, :, o, :].rearrange("p s g d -> p (s g) d")
+                source = pair_tiles[r][:, :, :, 3 * o, :].rearrange("p s g d -> p (s g) d")
+                if r < 2 or o == 0:
+                    nc.scalar.copy(out=to, in_=source)
+                else:
+                    nc.vector.tensor_copy(out=to, in_=source)
             outer_of[r] = outer
 
         def average_pairs(r):
@@ -285,7 +290,7 @@ def tile_ferminetoneelectronlayer_pa_kernel(
             for s in range(SPINS):
                 for grp in range(GROUPS):
                     pairs = pair_tiles[r][:, s, grp]
-                    if r < JOINED_TILES:
+                    if joined_tile(r):
                         joined = (pairs[:, 1:3, :], outer_of[r][:, s, grp])
                     else:
                         joined = (pairs[:, 0:2, :], pairs[:, 2:4, :])
@@ -385,6 +390,8 @@ def tile_ferminetoneelectronlayer_pa_kernel(
                 average_pairs(1)
                 group_pairs(1)
             if r + 2 < RANKS:
+                if joined_tile(r + 2):
+                    join_outer(r + 2)
                 average_pairs(r + 2)
             add_mixed(r)
             if r == 0:

from contextlib import ExitStack

import concourse.mybir as mybir
from concourse.masks import make_identity

F32 = mybir.dt.float32
BF16 = mybir.dt.bfloat16
I32 = mybir.dt.int32
U32 = mybir.dt.uint32
U8 = mybir.dt.uint8
FP8X4 = mybir.dt.float8_e4m3fn_x4
FP4X4 = mybir.dt.float4_e2m1fn_x4
ADD = mybir.AluOpType.add
ACT = mybir.ActivationFunctionType

P = 128
WALKERS = 64
SPINS = 2
RANKS = 8
D1 = 1024
D2 = 256
N_HALF = 512
HALVES = D1 // N_HALF
K_PASS = 512
GROUPS = 2
GROUP_WALKERS = WALKERS // GROUPS
ROWS = 2
PACK = 4

PASS_UNMIXED = 0
PASS_MIXED = 2
PASS_2E = 6
PASSES = 7

FLOPS = 2 * (WALKERS * 16 * D1 * D1 + WALKERS * SPINS * SPINS * D1 * D1 + WALKERS * 16 * SPINS * D2 * D1)


def tile_ferminetoneelectronlayer_pa_kernel(
    tc,
    in_1e,
    in_2e,
    w_unmixed_words,
    w_unmixed_scales,
    b_unmixed,
    w_mixed_words,
    w_mixed_scales,
    w_2e_words,
    w_2e_scales,
    out,
):
    nc = tc.nc
    with ExitStack() as ctx:
        const = ctx.enter_context(tc.tile_pool(name="const", bufs=1))
        keep = ctx.enter_context(tc.tile_pool(name="keep", bufs=1))
        pair_pool = ctx.enter_context(tc.tile_pool(name="pair_pool", bufs=RANKS))
        outer_pool = ctx.enter_context(tc.tile_pool(name="outer_pool", bufs=4))
        out_pool = ctx.enter_context(tc.tile_pool(name="out_pool", bufs=RANKS))
        rows_pool = ctx.enter_context(tc.tile_pool(name="rows_pool", bufs=5))
        work = ctx.enter_context(tc.tile_pool(name="work", bufs=2))
        totals_pool = ctx.enter_context(tc.tile_pool(name="totals_pool", bufs=6))
        psum_sums = ctx.enter_context(tc.psum_pool(name="psum_sums", bufs=2))
        psum_flip = ctx.enter_context(tc.psum_pool(name="psum_flip", bufs=2))
        psum_acc = ctx.enter_context(tc.psum_pool(name="psum_acc", bufs=4))
        ctx.enter_context(tc.manual_schedule())

        x1_rows = in_1e.flatten_outer_dims().rearrange("(q r) k -> q r k", r=RANKS)
        out_rows = out.flatten_outer_dims().rearrange("(q r) n -> q r n", r=RANKS)
        pair_rows = in_2e.rearrange("b (s r) (c j a) d -> b s r c j a d", s=SPINS, c=SPINS, a=ROWS)

        w_scales = keep.tile([P, PASSES, D1], U8, align_bytes=256)
        nc.vector.memset(w_scales[:].bitcast(I32), 0)
        ident_f32 = const.tile([P, P], F32)
        make_identity(nc, ident_f32[:])
        bias_row = keep.tile([P, D1], BF16)
        nc.gpsimd.memset(bias_row[:], 0.0)
        ones = const.tile([P, P], BF16)
        nc.gpsimd.memset(ones[:], 1.0)
        member = const.tile([P, GROUP_WALKERS], F32)
        nc.vector.tensor_reduce(
            out=member[:],
            in_=ident_f32[:].rearrange("p (b j) -> p b j", b=GROUP_WALKERS),
            axis=mybir.AxisListType.X,
            op=ADD,
        )
        averager = const.tile([P, GROUP_WALKERS], BF16)
        nc.vector.tensor_scalar_mul(out=averager[:], in0=member[:], scalar1=1.0 / RANKS)

        w_words = keep.tile([P, PASSES, 2 * D1], U8, align_bytes=256)
        x1 = keep.tile([P, RANKS, D1], BF16)
        pair_tiles = []

        def joined_tile(r):
            return r < 2 or r in (4, 6)


        scale_loads = [
            (
                w_scales[32 * quadrant : 32 * quadrant + 4, first : first + scales.shape[0], :].bitcast(I32),
                scales[:, 4 * quadrant : 4 * quadrant + 4, :].rearrange("g r n -> r g n").bitcast(I32),
            )
            for first, scales in (
                (PASS_UNMIXED, w_unmixed_scales),
                (PASS_2E, w_2e_scales),
                (PASS_MIXED, w_mixed_scales),
            )
            for quadrant in range(4)
        ]

        def load(to, source):
            nc.sync.dma_start(out=to, in_=source)

        def load_scales(first, last):
            for to, source in scale_loads[first:last]:
                load(to, source)

        def load_words(first, words):
            load(
                w_words[:, first : first + words.shape[0], :].bitcast(I32),
                words.rearrange("g p n -> p g n").bitcast(I32),
            )

        def load_pairs(r):
            pairs = pair_pool.tile([P, SPINS, GROUPS, SPINS * ROWS, D2], BF16)
            for s in range(SPINS):
                for grp in range(GROUPS):
                    for o in range(SPINS):
                        rows = slice(ROWS * o, ROWS * (o + 1)) if joined_tile(r) else slice(o, SPINS * ROWS, SPINS)
                        load(
                            pairs[:, s, grp, rows, :],
                            pair_rows[GROUP_WALKERS * grp : GROUP_WALKERS * (grp + 1), s, r, (s + o) % SPINS],
                        )
            pair_tiles.append(pairs)

        for r in range(0, RANKS, 2):
            nc.sync.dma_start(out=x1[:, r : r + 2, :], in_=x1_rows[:, r : r + 2, :])
        load_scales(0, 4)
        nc.sync.dma_start(out=bias_row[0:1, :], in_=b_unmixed.unsqueeze(0))
        load_words(PASS_UNMIXED, w_unmixed_words)
        load_words(PASS_2E, w_2e_words)
        load_scales(4, 6)
        load_pairs(0)
        load_words(PASS_MIXED + 0, w_mixed_words[0 : 2])
        load_scales(6, 9)
        load_words(PASS_MIXED + 2, w_mixed_words[2 : 4])
        load_scales(9, 12)
        for r in range(1, RANKS):
            load_pairs(r)

        def mx_pass(acc, codes, scales, w_pass, half, start, stop):
            nc.tensor.matmul_mx(
                out=acc,
                lhsT=codes.bitcast(FP8X4),
                lhsT_scale=scales,
                rhs=w_words[:, w_pass, 2 * N_HALF * half : 2 * N_HALF * (half + 1)].bitcast(FP4X4),
                rhs_scale=w_scales[:, w_pass, N_HALF * half : N_HALF * (half + 1)],
                start=start,
                stop=stop,
            )

        x1_grouped = keep.tile([P, RANKS, 2 * K_PASS], BF16, align_bytes=64)
        x1_codes = keep.tile([P, RANKS, 2 * P], U32, align_bytes=256)
        x1_scales = keep.tile([P, RANKS, 2 * P], U8, align_bytes=256)

        def turn_x1(r, flipped, copy):
            x1_words = x1[:, r, :].bitcast(F32)
            for g in range(2):
                for u in range(2):
                    nc.tensor.transpose(
                        flipped[:, g, u, :],
                        x1_words[:, 256 * g + u : 256 * (g + 1) : 2],
                        ident_f32[:],
                    )
            copy(
                out=x1_grouped[:, r, :].bitcast(F32).rearrange("p (g q u) -> p g q u", g=2, u=2),
                in_=flipped[:].rearrange("p g u q -> p g q u"),
            )

        def quantise_x1(r, tiles):
            nc.vector.quantize_mx(
                out=x1_codes[:, r : r + tiles, :].rearrange("p r q -> p (r q)").bitcast(FP8X4),
                scales=x1_scales[:, r : r + tiles, :].rearrange("p r q -> p (r q)"),
                in_=x1_grouped[:, r : r + tiles, :].rearrange("p r k -> p (r k)"),
            )

        running = keep.tile([P, D1], F32)
        spins_grouped = keep.tile([P, SPINS, 2, P, PACK], BF16, align_bytes=64)
        spins_codes = keep.tile([P, SPINS, 2 * P], U32, align_bytes=256)
        spins_scales = keep.tile([P, SPINS, 2 * P], U8, align_bytes=256)
        mixed = keep.tile([P, D1], F32)

        def add_rows(r, flipped):
            two_rows = rows_pool.tile([P, 2, P, 2, 2], F32, tag="rows")
            for g in range(2):
                nc.vector.tensor_tensor(
                    out=two_rows[:, g],
                    in0=flipped[:, g].bitcast(BF16).rearrange("p u (q e) -> p q u e", e=2),
                    in1=x1_grouped[:, r, K_PASS * g : K_PASS * (g + 1)].rearrange("p (q u e) -> p q u e", u=2, e=2),
                    op=ADD,
                )
            return two_rows[:].rearrange("p g q u e -> p (g q u e)")

        pair_rows_of = []
        for r in range(0, RANKS, 2):
            even = psum_flip.tile([P, 2, 2, P], F32, tag="flip")
            copy = nc.vector.tensor_copy if r == 0 else nc.scalar.copy
            turn_x1(r, even, copy)
            odd = psum_acc.tile([P, 2, 2, P], F32, tag="acc")
            turn_x1(r + 1, odd, copy)
            if r % 4 == 0:
                two_rows = rows_pool.tile([P, D1], F32, tag="rows")
                nc.gpsimd.tensor_tensor(out=two_rows[:], in0=x1_grouped[:, r, :], in1=x1_grouped[:, r + 1, :], op=ADD)
                pair_rows_of.append(two_rows[:])
            else:
                pair_rows_of.append(add_rows(r, odd))
            if r == 2:
                quantise_x1(0, 2)
        own = spins_grouped[:, 0].rearrange("p g q t -> p (g q t)")
        nc.vector.tensor_tensor(out=running[:], in0=pair_rows_of[0], in1=pair_rows_of[1], op=ADD)
        last_rows = rows_pool.tile([P, D1], F32, tag="rows")
        nc.vector.tensor_tensor(out=last_rows[:], in0=pair_rows_of[2], in1=pair_rows_of[3], op=ADD)
        nc.vector.tensor_tensor(out=own, in0=running[:], in1=last_rows[:], op=ADD)

        def quantise_spin(o):
            nc.vector.quantize_mx(
                out=spins_codes[:, o, :].bitcast(FP8X4),
                scales=spins_scales[:, o, :],
                in_=spins_grouped[:, o].rearrange("p g q t -> p (g q t)"),
            )

        def quantise_spins():
            quantise_spin(0)
            for s, copy in enumerate((nc.vector.tensor_copy, nc.scalar.copy)):
                copy(
                    out=spins_grouped[:, 1].rearrange("p g (b s) t -> p g b s t", s=SPINS)[:, :, :, s, :],
                    in_=spins_grouped[:, 0].rearrange("p g (b s) t -> p g b s t", s=SPINS)[:, :, :, 1 - s, :],
                )
            quantise_spin(1)

        def spread_bias():
            for half in range(HALVES):
                cols = slice(N_HALF * half, N_HALF * (half + 1))
                bias_acc = psum_flip.tile([P, N_HALF], F32, tag="flip")
                nc.tensor.matmul(out=bias_acc[:], lhsT=ones[:], rhs=bias_row[:, cols], start=True, stop=True)
                nc.scalar.copy(out=mixed[:, cols], in_=bias_acc[:])

        def mixed_term():
            accs = [psum_flip.tile([P, N_HALF], F32, name="mixed_acc", tag="flip") for half in range(HALVES)]
            for o in range(SPINS):
                for half in range(HALVES):
                    for g in range(2):
                        mx_pass(
                            accs[half][:],
                            spins_codes[:, o, P * g : P * (g + 1)],
                            spins_scales[:, o, P * g : P * (g + 1)],
                            PASS_MIXED + 2 * o + g,
                            half,
                            o + g == 0,
                            o + g == 2,
                        )
            for half in range(HALVES):
                cols = slice(N_HALF * half, N_HALF * (half + 1))
                nc.vector.scalar_tensor_tensor(
                    out=mixed[:, cols],
                    in0=accs[half][:],
                    scalar=1.0 / RANKS,
                    in1=mixed[:, cols],
                    op0=mybir.AluOpType.mult,
                    op1=ADD,
                )

        pair_codes = keep.tile([P, RANKS, P], U32, align_bytes=256)
        pair_scales = keep.tile([P, RANKS, P], U8, align_bytes=256)
        pair_sums_of = {}

        outer_of = {}

        def join_outer(r):
            outer = outer_pool.tile([P, SPINS, GROUPS, SPINS, D2], BF16)
            for o in range(SPINS):
                to = outer[:, :, :, o, :].rearrange("p s g d -> p (s g) d")
                source = pair_tiles[r][:, :, :, 3 * o, :].rearrange("p s g d -> p (s g) d")
                if r < 2 or o == 0:
                    nc.scalar.copy(out=to, in_=source)
                else:
                    nc.vector.tensor_copy(out=to, in_=source)
            outer_of[r] = outer

        def average_pairs(r):
            pair_sums = psum_sums.tile([P, PACK, SPINS, WALKERS], F32)
            for s in range(SPINS):
                for grp in range(GROUPS):
                    pairs = pair_tiles[r][:, s, grp]
                    if joined_tile(r):
                        joined = (pairs[:, 1:3, :], outer_of[r][:, s, grp])
                    else:
                        joined = (pairs[:, 0:2, :], pairs[:, 2:4, :])
                    for t in range(PACK):
                        for a in range(ROWS):
                            nc.tensor.matmul(
                                out=pair_sums[:, t, s, GROUP_WALKERS * grp : GROUP_WALKERS * (grp + 1)],
                                lhsT=joined[a].rearrange("p o d -> p (o d)")[:, t : SPINS * D2 : PACK],
                                rhs=averager[:],
                                start=(a == 0),
                                stop=(a == ROWS - 1),
                            )
            pair_sums_of[r] = pair_sums

        pair_grouped_of = {}

        def group_pairs(r):
            pair_grouped = work.tile([P, WALKERS, SPINS, PACK], BF16, align_bytes=64)
            nc.scalar.copy(out=pair_grouped[:], in_=pair_sums_of[r][:].rearrange("p t s b -> p b s t"))
            pair_grouped_of[r] = pair_grouped

        def quantise_pairs(r):
            nc.vector.quantize_mx(
                out=pair_codes[:, r, :].bitcast(FP8X4),
                scales=pair_scales[:, r, :],
                in_=pair_grouped_of[r][:].rearrange("p b s t -> p (b s t)"),
            )

        acc_of = {}
        totals_of = {}

        def start_half(r, half):
            acc = psum_acc.tile([P, N_HALF], F32, tag="acc")
            for g in range(2):
                mx_pass(
                    acc[:],
                    x1_codes[:, r, P * g : P * (g + 1)],
                    x1_scales[:, r, P * g : P * (g + 1)],
                    PASS_UNMIXED + g,
                    half,
                    g == 0,
                    False,
                )
            acc_of[r, half] = acc

        def start_tile(r):
            for half in range(HALVES):
                start_half(r, half)

        def add_pairs(r, half):
            acc = acc_of[r, half]
            mx_pass(acc[:], pair_codes[:, r, :], pair_scales[:, r, :], PASS_2E, half, False, True)

        def add_mixed(r):
            totals = []
            for half in range(HALVES):
                total = totals_pool.tile([P, N_HALF], F32)
                nc.vector.tensor_tensor(
                    out=total[:], in0=acc_of[r, half][:], in1=mixed[:, N_HALF * half : N_HALF * (half + 1)], op=ADD
                )
                nc.scalar.activation(out=total[:], in_=total[:], func=ACT.Tanh)
                totals.append(total)
            totals_of[r] = totals

        def add_skip(r):
            result = out_pool.tile([P, D1], F32)
            by_half = r >= RANKS - 3
            for half in range(HALVES):
                cols = slice(N_HALF * half, N_HALF * (half + 1))
                adder = nc.gpsimd if half == 0 and RANKS - 3 <= r < RANKS - 1 else nc.vector
                adder.tensor_tensor(out=result[:, cols], in0=totals_of[r][half][:], in1=x1[:, r, cols], op=ADD)
                if by_half:
                    nc.sync.dma_start(out=out_rows[:, r, cols], in_=result[:, cols])
            if not by_half:
                nc.sync.dma_start(out=out_rows[:, r, :], in_=result[:])

        spread_bias()
        start_tile(0)
        start_tile(1)
        join_outer(0)
        average_pairs(0)
        quantise_spins()
        group_pairs(0)
        quantise_x1(2, 2)
        quantise_pairs(0)
        mixed_term()
        quantise_x1(4, 4)
        join_outer(1)
        for r in range(RANKS):
            for half in range(HALVES):
                if r == RANKS - 1:
                    start_half(r, half)
                add_pairs(r, half)
            if 0 < r < RANKS - 2:
                start_tile(r + 1)
            if r == 0:
                average_pairs(1)
                group_pairs(1)
            if r + 2 < RANKS:
                if joined_tile(r + 2):
                    join_outer(r + 2)
                average_pairs(r + 2)
            add_mixed(r)
            if r == 0:
                quantise_pairs(1)
            if r > 0:
                add_skip(r - 1)
            if r + 2 < RANKS:
                group_pairs(r + 2)
                quantise_pairs(r + 2)
        add_skip(RANKS - 1)
